import numpy as np
import ml_dtypes


def mxq(x, axis, fmt="e4m3"):
    dtype, down = {"e4m3": (ml_dtypes.float8_e4m3fn, 7), "e5m2": (ml_dtypes.float8_e5m2, 14)}[fmt]
    v = np.moveaxis(np.asarray(x, np.float32).astype(ml_dtypes.bfloat16).astype(np.float64), axis, -1)
    blocks = v.reshape(v.shape[:-1] + (-1, 32))
    amax = np.abs(blocks).max(-1, keepdims=True)
    byte = np.maximum(np.where(amax > 0, np.frexp(amax)[1] - 1 + 127, 0) - down, 1)
    scale = np.exp2(byte - 127.0)
    codes = (blocks / scale).astype(np.float32).astype(dtype).astype(np.float64)
    return np.moveaxis((codes * scale).reshape(v.shape), -1, axis)


WIDE = False


def mx_kscale(k):
    if not WIDE:
        return np.ones(k)
    levels = np.array([10, -10, 5, -5, 0])
    a = np.random.permutation(np.resize(levels, k // 512 * 4)).reshape(k // 512, 4)
    idx = np.arange(k)
    return np.exp2(a[idx // 512, idx % 128 // 32])


BF16 = ml_dtypes.bfloat16


def bf(x):
    return np.asarray(x, np.float32).astype(BF16)


def f64(x):
    return np.asarray(x).astype(np.float64)


E2M1 = np.array([0.0, 0.5, 1.0, 1.5, 2.0, 3.0, 4.0, 6.0, -0.0, -0.5, -1.0, -1.5, -2.0, -3.0, -4.0, -6.0])


def pack_weight(w, fmt):
    k, n = w.shape
    w = f64(bf(w)).reshape(k // 32, 32, n)
    amax = np.abs(w).max(1)
    if fmt == "e4m3":
        byte = np.frexp(amax)[1] - 1 + 127 - 7
    else:
        mant, ex = np.frexp(amax / 6.0)
        byte = np.where(mant > 0.5, ex, ex - 1) + 127
    byte = np.clip(np.where(amax > 0, byte, 1), 1, 254)
    scaled = (w * np.exp2(127.0 - byte)[:, None, :]).reshape(k, n).astype(np.float32)
    by_word = np.ascontiguousarray(scaled.reshape(k // 512, 128, 4, n).transpose(0, 1, 3, 2))
    if fmt == "e4m3":
        words = by_word.astype(ml_dtypes.float8_e4m3fn).view(np.uint8)
    else:
        c = by_word.astype(ml_dtypes.float4_e2m1fn).view(np.uint8) & 0xF
        words = c[..., 0::2] | (c[..., 1::2] << 4)
    return np.ascontiguousarray(words), np.ascontiguousarray(byte.astype(np.uint8).reshape(k // 512, 16, n))


def unpack_weight(words, scales, fmt):
    g, p, n, _ = words.shape
    if fmt == "e4m3":
        vals = np.ascontiguousarray(words).view(ml_dtypes.float8_e4m3fn).astype(np.float64)
    else:
        nib = np.empty((g, p, n, 4), np.uint8)
        nib[..., 0::2] = words & 0xF
        nib[..., 1::2] = words >> 4
        vals = E2M1[nib]
    vals = vals * np.repeat(np.exp2(scales.astype(np.float64) - 127.0), 8, axis=1)[..., None]
    return vals.transpose(0, 1, 3, 2).reshape(g * 512, n)


B, T, C, NH, NC = 4, 1024, 512, 4, 2
HS = C // NH
N = T // NC
FMT = "e4m3"


def setup_inputs():
    s = mx_kscale(T)
    q = bf(np.random.standard_normal((B, NH, T, HS)) * 2.0)
    k_mix = bf(np.random.standard_normal((B, NH, T, HS)))
    v_heads = bf(np.random.standard_normal((B, NH, T, HS)) * s[:, None])
    stack = np.random.standard_normal((NC, N, N)) / np.sqrt(N) / s.reshape(NC, 1, N)
    cat = np.ascontiguousarray(stack.swapaxes(1, 2)).reshape(-1, N)
    words, scales = pack_weight(cat, FMT)
    pv_b = bf(np.random.standard_normal((NC, N)) * 0.3)
    return {"q": q,
            "k_mix": k_mix,
            "v_heads": v_heads,
            "pv_W_words": words,
            "pv_W_scales": scales,
            "pv_b": pv_b}


def reference(q, k_mix, v_heads, pv_W_words, pv_W_scales, pv_b):
    vh = f64(v_heads).reshape(B, NH, NC, N, HS)
    pw = unpack_weight(pv_W_words, pv_W_scales, FMT).reshape(NC, N, N).swapaxes(1, 2)
    vm = ((pw @ mxq(vh, 3, "e4m3")) + f64(pv_b)[:, :, None]).reshape(B, NH, T, HS)
    s = f64(q) @ f64(k_mix).transpose(0, 1, 3, 2) / np.sqrt(HS)
    e = np.exp(s - s.max(-1, keepdims=True))
    y = (mxq(e, 3, "e4m3") @ mxq(vm, 2, "e4m3")) / e.sum(-1, keepdims=True)
    return y.transpose(0, 2, 1, 3).reshape(B, T, C)

@@ -1,0 +1,243 @@
+from contextlib import ExitStack
+import math
+
+from concourse import mybir
+from concourse.masks import make_identity
+
+BF16 = mybir.dt.bfloat16
+F32 = mybir.dt.float32
+I32 = mybir.dt.int32
+U32 = mybir.dt.uint32
+U8 = mybir.dt.uint8
+FP8X4 = mybir.dt.float8_e4m3fn_x4
+ALU = mybir.AluOpType
+ACT = mybir.ActivationFunctionType
+AXIS_X = mybir.AxisListType.X
+
+P = 128
+PACK = 4
+K_PASS = P * PACK
+B, NH, T, HS = 4, 4, 1024, 128
+HEADS = B * NH
+CHUNKS = T // K_PASS
+Q_TILES = T // P
+Y_GROUP = 4
+SCALE = 1.0 / math.sqrt(HS)
+
+FLOPS = 2 * HEADS * (T * K_PASS * HS + 2 * T * T * HS)
+
+
+def tile_causalselfattention_pb_t_e_kernel(
+    tc, q, k_mix, v_heads, pv_W_words, pv_W_scales, pv_b, out
+):
+    nc = tc.nc
+    with ExitStack() as stack:
+        const = stack.enter_context(tc.tile_pool(name="const", bufs=1))
+        inputs = stack.enter_context(tc.tile_pool(name="inputs", bufs=1))
+        head = stack.enter_context(tc.tile_pool(name="head", bufs=2))
+        work = stack.enter_context(tc.tile_pool(name="work", bufs=3))
+        psum = stack.enter_context(tc.psum_pool(name="psum", bufs=1))
+
+        ident_bf = const.tile([P, P], BF16)
+        make_identity(nc, ident_bf[:])
+        ident_f32 = const.tile([P, P], F32)
+        make_identity(nc, ident_f32[:])
+
+        w_words = const.tile([P, CHUNKS, K_PASS], U32, align_bytes=64)
+        w_scales = const.tile([P, CHUNKS, K_PASS], U8, align_bytes=64)
+        nc.vector.memset(w_scales[:].bitcast(I32), 0)
+        for c in range(CHUNKS):
+            nc.sync.dma_start(
+                out=w_words[:, c, :].bitcast(I32),
+                in_=pv_W_words[c].rearrange("p m t -> p (m t)").bitcast(I32),
+            )
+            for quad in range(4):
+                nc.sync.dma_start(
+                    out=w_scales[32 * quad : 32 * quad + 4, c, :].bitcast(I32),
+                    in_=pv_W_scales[c, 4 * quad : 4 * quad + 4, :].bitcast(I32),
+                )
+
+        b_rows = const.tile([P, P], BF16)
+        nc.vector.memset(b_rows[:], 0.0)
+        nc.sync.dma_start(
+            out=b_rows[0 : CHUNKS * PACK, :], in_=pv_b.rearrange("c (t i) -> (c t) i", i=P)
+        )
+        b_ps = psum.tile([P, T], BF16, tag="prep")
+        nc.tensor.transpose(out=b_ps[:, 0:P], in_=b_rows[:], identity=ident_bf[:])
+        bias = const.tile([P, CHUNKS * PACK], F32)
+        nc.vector.tensor_copy(out=bias[:], in_=b_ps[:, 0 : CHUNKS * PACK])
+
+        k_sb, q_sb, v_sb = [], [], []
+        for h in range(HEADS):
+            bi, hi = divmod(h, NH)
+            k_t = inputs.tile([P, Q_TILES, HS], BF16, name="k_sb%d" % h)
+            nc.sync.dma_start(out=k_t[:], in_=k_mix[bi, hi].rearrange("(n p) d -> p n d", p=P))
+            q_t = inputs.tile([P, Q_TILES, HS], BF16, name="q_sb%d" % h)
+            nc.sync.dma_start(out=q_t[:], in_=q[bi, hi].rearrange("(p n) d -> p n d", n=Q_TILES))
+            v_t = inputs.tile([P, CHUNKS, PACK, HS], BF16, name="v_sb%d" % h)
+            nc.sync.dma_start(
+                out=v_t[:], in_=v_heads[bi, hi].rearrange("(c p j) d -> p c j d", p=P, j=PACK)
+            )
+            k_sb.append(k_t)
+            q_sb.append(q_t)
+            v_sb.append(v_t)
+
+        def transpose_head(src):
+            ps = psum.tile([P, T], BF16, tag="prep")
+            for n in range(Q_TILES):
+                nc.tensor.transpose(
+                    out=ps[:, n * P : (n + 1) * P], in_=src[:, n, :], identity=ident_bf[:]
+                )
+            return ps
+
+        def prepare_qk(h):
+            kT = head.tile([P, T], BF16, tag="kT")
+            nc.scalar.copy(out=kT[:], in_=transpose_head(k_sb[h])[:])
+            qT = head.tile([P, T], BF16, tag="qT")
+            nc.scalar.copy(out=qT[:], in_=transpose_head(q_sb[h])[:])
+            return qT, kT
+
+        def prepare_vm(h):
+            v_grouped = head.tile([P, CHUNKS, HS, PACK], BF16, tag="v_grouped", align_bytes=64)
+            nc.gpsimd.tensor_scalar(
+                out=v_grouped[:],
+                in0=v_sb[h][:].rearrange("p c j d -> p c d j"),
+                scalar1=1.0,
+                scalar2=0.0,
+                op0=ALU.mult,
+                op1=ALU.add,
+            )
+            v_codes = head.tile([P, CHUNKS, HS], U32, tag="v_codes", align_bytes=64)
+            v_scales = head.tile([P, CHUNKS, HS], U8, tag="v_scales", align_bytes=64)
+            nc.vector.quantize_mx(
+                out=v_codes[:].rearrange("p c d -> p (c d)").bitcast(FP8X4),
+                scales=v_scales[:].rearrange("p c d -> p (c d)"),
+                in_=v_grouped[:].rearrange("p c d j -> p (c d j)"),
+            )
+            vm_grouped = head.tile([P, CHUNKS, HS, PACK], BF16, tag="vm_grouped", align_bytes=64)
+            for c in range(CHUNKS):
+                vm_ps = psum.tile([P, PACK, HS], F32, tag="prep")
+                for t in range(PACK):
+                    m_cols = slice(t * P, (t + 1) * P)
+                    nc.tensor.matmul_mx(
+                        out=vm_ps[:, t, :],
+                        lhsT=w_words[:, c, m_cols].bitcast(FP8X4),
+                        lhsT_scale=w_scales[:, c, m_cols],
+                        rhs=v_codes[:, c, :].bitcast(FP8X4),
+                        rhs_scale=v_scales[:, c, :],
+                        start=True,
+                        stop=True,
+                    )
+                nc.vector.tensor_tensor(
+                    out=vm_grouped[:, c, :, :],
+                    in0=vm_ps[:].rearrange("p t d -> p d t"),
+                    in1=bias[:, c * PACK : (c + 1) * PACK].unsqueeze(1).to_broadcast([P, HS, PACK]),
+                    op=ALU.add,
+                )
+            vm_codes = head.tile([P, CHUNKS, HS], U32, tag="vm_codes", align_bytes=64)
+            vm_scales = head.tile([P, CHUNKS, HS], U8, tag="vm_scales", align_bytes=64)
+            nc.vector.quantize_mx(
+                out=vm_codes[:].rearrange("p c d -> p (c d)").bitcast(FP8X4),
+                scales=vm_scales[:].rearrange("p c d -> p (c d)"),
+                in_=vm_grouped[:].rearrange("p c d t -> p (c d t)"),
+            )
+            return vm_codes, vm_scales
+
+        def attend(qT, kT, vm_codes, vm_scales, n, y_ps, row_sums):
+            j = n % Y_GROUP
+            s_ps = []
+            half_max = work.tile([P, CHUNKS], F32, tag="half_max")
+            for g in range(CHUNKS):
+                s_g = psum.tile([P, K_PASS], F32, tag="s", bufs=4, name="s_g")
+                nc.tensor.matmul(
+                    out=s_g[:],
+                    lhsT=qT[:, n * P : (n + 1) * P],
+                    rhs=kT[:, g * K_PASS : (g + 1) * K_PASS],
+                    start=True,
+                    stop=True,
+                )
+                nc.vector.tensor_reduce(out=half_max[:, g : g + 1], in_=s_g[:], axis=AXIS_X, op=ALU.max)
+                s_ps.append(s_g)
+            shift = work.tile([P, 1], F32, tag="shift")
+            nc.vector.tensor_scalar(
+                out=shift[:],
+                in0=half_max[:, 0:1],
+                scalar1=half_max[:, 1:2],
+                scalar2=-SCALE,
+                op0=ALU.max,
+                op1=ALU.mult,
+            )
+            e_sb = work.tile([P, T], BF16, tag="e_sb")
+            for g in range(CHUNKS):
+                nc.scalar.activation(
+                    out=e_sb[:, g * K_PASS : (g + 1) * K_PASS].rearrange(
+                        "q (u p e) -> q u p e", u=2, e=2
+                    ),
+                    in_=s_ps[g][:].rearrange("q (u e p) -> q u p e", u=2, e=2),
+                    func=ACT.Exp,
+                    bias=shift[:, 0:1],
+                    scale=SCALE,
+                    accum_out=row_sums[:, j, g : g + 1],
+                )
+            eT_ps = psum.tile([P, 2 * CHUNKS, P], F32, tag="eT", bufs=2)
+            e_words = e_sb[:].bitcast(F32)
+            for w in range(2 * CHUNKS):
+                nc.tensor.transpose(
+                    out=eT_ps[:, w, :], in_=e_words[:, w * P : (w + 1) * P], identity=ident_f32[:]
+                )
+            e_grouped = work.tile([P, T], BF16, tag="e_grouped", align_bytes=64)
+            nc.scalar.copy(
+                out=e_grouped[:].bitcast(F32).rearrange("p (g q u) -> p g q u", g=CHUNKS, u=2),
+                in_=eT_ps[:].rearrange("p (g u) q -> p g q u", u=2),
+            )
+            e_codes = work.tile([P, CHUNKS * P], U32, tag="e_codes", align_bytes=64)
+            e_scales = work.tile([P, CHUNKS * P], U8, tag="e_scales", align_bytes=64)
+            nc.vector.quantize_mx(out=e_codes[:].bitcast(FP8X4), scales=e_scales[:], in_=e_grouped[:])
+            for g in range(CHUNKS):
+                q_cols = slice(g * P, (g + 1) * P)
+                nc.tensor.matmul_mx(
+                    out=y_ps[:, j, :],
+                    lhsT=e_codes[:, q_cols].bitcast(FP8X4),
+                    lhsT_scale=e_scales[:, q_cols],
+                    rhs=vm_codes[:, g, :].bitcast(FP8X4),
+                    rhs_scale=vm_scales[:, g, :],
+                    start=(g == 0),
+                    stop=(g == CHUNKS - 1),
+                )
+
+        def normalise_and_store(h, first_n, y_ps, row_sums):
+            bi, hi = divmod(h, NH)
+            row_sum = work.tile([P, Y_GROUP], F32, tag="row_sum")
+            nc.vector.tensor_reduce(out=row_sum[:], in_=row_sums[:], axis=AXIS_X, op=ALU.add)
+            inv_sum = work.tile([P, Y_GROUP], F32, tag="inv_sum")
+            nc.vector.reciprocal(out=inv_sum[:], in_=row_sum[:])
+            y_sb = work.tile([P, Y_GROUP, HS], F32, tag="y_sb")
+            nc.vector.tensor_tensor(
+                out=y_sb[:],
+                in0=y_ps[:],
+                in1=inv_sum[:].unsqueeze(2).to_broadcast([P, Y_GROUP, HS]),
+                op=ALU.mult,
+            )
+            nc.sync.dma_start(
+                out=out[bi].rearrange("(p n) c -> p n c", n=Q_TILES)[
+                    :, first_n : first_n + Y_GROUP, hi * HS : (hi + 1) * HS
+                ],
+                in_=y_sb[:],
+            )
+
+        qk = prepare_qk(0)
+        vm = prepare_vm(0)
+        for h in range(HEADS):
+            next_qk, next_vm = None, None
+            for n in range(Q_TILES):
+                if n % Y_GROUP == 0:
+                    y_ps = psum.tile([P, Y_GROUP, HS], F32, tag="y")
+                    row_sums = work.tile([P, Y_GROUP, CHUNKS], F32, tag="row_sums")
+                attend(qk[0], qk[1], vm[0], vm[1], n, y_ps, row_sums)
+                if n % Y_GROUP == Y_GROUP - 1:
+                    normalise_and_store(h, n - (Y_GROUP - 1), y_ps, row_sums)
+                if h + 1 < HEADS and n == 2:
+                    next_qk = prepare_qk(h + 1)
+                if h + 1 < HEADS and n == 5:
+                    next_vm = prepare_vm(h + 1)
+            qk, vm = next_qk, next_vm

@@ -1,7 +1,7 @@
 from contextlib import ExitStack
 import math
 
-from concourse import mybir
+import concourse.mybir as mybir
 from concourse.masks import make_identity
 
 BF16 = mybir.dt.bfloat16
@@ -22,6 +22,7 @@ HEADS = B * NH
 CHUNKS = T // K_PASS
 Q_TILES = T // P
 Y_GROUP = 4
+UNITS = HEADS * Q_TILES
 SCALE = 1.0 / math.sqrt(HS)
 
 FLOPS = 2 * HEADS * (T * K_PASS * HS + 2 * T * T * HS)
@@ -37,6 +38,22 @@ def tile_causalselfattention_pb_t_e_kernel(
         head = stack.enter_context(tc.tile_pool(name="head", bufs=2))
         work = stack.enter_context(tc.tile_pool(name="work", bufs=3))
         psum = stack.enter_context(tc.psum_pool(name="psum", bufs=1))
+        stack.enter_context(tc.manual_schedule())
+
+        k_sb, q_sb, v_sb = {}, {}, {}
+
+        def load_head(h):
+            bi, hi = divmod(h, NH)
+            k_sb[h] = inputs.tile([P, Q_TILES, HS], BF16, name="k_sb%d" % h)
+            nc.sync.dma_start(out=k_sb[h][:], in_=k_mix[bi, hi].rearrange("(n p) d -> p n d", p=P))
+            q_sb[h] = inputs.tile([P, Q_TILES, HS], BF16, name="q_sb%d" % h)
+            nc.sync.dma_start(out=q_sb[h][:], in_=q[bi, hi].rearrange("(p n) d -> p n d", n=Q_TILES))
+            v_sb[h] = inputs.tile([P, CHUNKS, PACK, HS], BF16, name="v_sb%d" % h)
+            nc.sync.dma_start(
+                out=v_sb[h][:], in_=v_heads[bi, hi].rearrange("(c p j) d -> p c j d", p=P, j=PACK)
+            )
+
+        load_head(0)
 
         ident_bf = const.tile([P, P], BF16)
         make_identity(nc, ident_bf[:])
@@ -46,6 +63,8 @@ def tile_causalselfattention_pb_t_e_kernel(
         w_words = const.tile([P, CHUNKS, K_PASS], U32, align_bytes=64)
         w_scales = const.tile([P, CHUNKS, K_PASS], U8, align_bytes=64)
         nc.vector.memset(w_scales[:].bitcast(I32), 0)
+        b_rows = const.tile([P, P], BF16)
+        nc.vector.memset(b_rows[:], 0.0)
         for c in range(CHUNKS):
             nc.sync.dma_start(
                 out=w_words[:, c, :].bitcast(I32),
@@ -56,48 +75,26 @@ def tile_causalselfattention_pb_t_e_kernel(
                     out=w_scales[32 * quad : 32 * quad + 4, c, :].bitcast(I32),
                     in_=pv_W_scales[c, 4 * quad : 4 * quad + 4, :].bitcast(I32),
                 )
-
-        b_rows = const.tile([P, P], BF16)
-        nc.vector.memset(b_rows[:], 0.0)
         nc.sync.dma_start(
             out=b_rows[0 : CHUNKS * PACK, :], in_=pv_b.rearrange("c (t i) -> (c t) i", i=P)
         )
-        b_ps = psum.tile([P, T], BF16, tag="prep")
-        nc.tensor.transpose(out=b_ps[:, 0:P], in_=b_rows[:], identity=ident_bf[:])
-        bias = const.tile([P, CHUNKS * PACK], F32)
-        nc.vector.tensor_copy(out=bias[:], in_=b_ps[:, 0 : CHUNKS * PACK])
+        for h in range(1, HEADS):
+            load_head(h)
 
-        k_sb, q_sb, v_sb = [], [], []
-        for h in range(HEADS):
-            bi, hi = divmod(h, NH)
-            k_t = inputs.tile([P, Q_TILES, HS], BF16, name="k_sb%d" % h)
-            nc.sync.dma_start(out=k_t[:], in_=k_mix[bi, hi].rearrange("(n p) d -> p n d", p=P))
-            q_t = inputs.tile([P, Q_TILES, HS], BF16, name="q_sb%d" % h)
-            nc.sync.dma_start(out=q_t[:], in_=q[bi, hi].rearrange("(p n) d -> p n d", n=Q_TILES))
-            v_t = inputs.tile([P, CHUNKS, PACK, HS], BF16, name="v_sb%d" % h)
-            nc.sync.dma_start(
-                out=v_t[:], in_=v_heads[bi, hi].rearrange("(c p j) d -> p c j d", p=P, j=PACK)
-            )
-            k_sb.append(k_t)
-            q_sb.append(q_t)
-            v_sb.append(v_t)
+        prep_ps, qT, kT, v_mx, vm_grouped, vm_mx = {}, {}, {}, {}, {}, {}
 
-        def transpose_head(src):
-            ps = psum.tile([P, T], BF16, tag="prep")
+        def transpose_tokens(src):
+            prep_ps[0] = psum.tile([P, T], BF16, tag="prep", name="tokens_ps")
             for n in range(Q_TILES):
                 nc.tensor.transpose(
-                    out=ps[:, n * P : (n + 1) * P], in_=src[:, n, :], identity=ident_bf[:]
+                    out=prep_ps[0][:, n * P : (n + 1) * P], in_=src[:, n, :], identity=ident_bf[:]
                 )
-            return ps
 
-        def prepare_qk(h):
-            kT = head.tile([P, T], BF16, tag="kT")
-            nc.scalar.copy(out=kT[:], in_=transpose_head(k_sb[h])[:])
-            qT = head.tile([P, T], BF16, tag="qT")
-            nc.scalar.copy(out=qT[:], in_=transpose_head(q_sb[h])[:])
-            return qT, kT
+        def keep_transposed(dest, h, tag):
+            dest[h] = head.tile([P, T], BF16, tag=tag, name=tag)
+            nc.scalar.copy(out=dest[h][:], in_=prep_ps[0][:])
 
-        def prepare_vm(h):
+        def quantise_v(h):
             v_grouped = head.tile([P, CHUNKS, HS, PACK], BF16, tag="v_grouped", align_bytes=64)
             nc.gpsimd.tensor_scalar(
                 out=v_grouped[:],
@@ -107,114 +104,161 @@ def tile_causalselfattention_pb_t_e_kernel(
                 op0=ALU.mult,
                 op1=ALU.add,
             )
-            v_codes = head.tile([P, CHUNKS, HS], U32, tag="v_codes", align_bytes=64)
-            v_scales = head.tile([P, CHUNKS, HS], U8, tag="v_scales", align_bytes=64)
-            nc.vector.quantize_mx(
-                out=v_codes[:].rearrange("p c d -> p (c d)").bitcast(FP8X4),
-                scales=v_scales[:].rearrange("p c d -> p (c d)"),
-                in_=v_grouped[:].rearrange("p c d j -> p (c d j)"),
-            )
-            vm_grouped = head.tile([P, CHUNKS, HS, PACK], BF16, tag="vm_grouped", align_bytes=64)
-            for c in range(CHUNKS):
-                vm_ps = psum.tile([P, PACK, HS], F32, tag="prep")
-                for t in range(PACK):
-                    m_cols = slice(t * P, (t + 1) * P)
-                    nc.tensor.matmul_mx(
-                        out=vm_ps[:, t, :],
-                        lhsT=w_words[:, c, m_cols].bitcast(FP8X4),
-                        lhsT_scale=w_scales[:, c, m_cols],
-                        rhs=v_codes[:, c, :].bitcast(FP8X4),
-                        rhs_scale=v_scales[:, c, :],
-                        start=True,
-                        stop=True,
-                    )
-                nc.vector.tensor_tensor(
-                    out=vm_grouped[:, c, :, :],
-                    in0=vm_ps[:].rearrange("p t d -> p d t"),
-                    in1=bias[:, c * PACK : (c + 1) * PACK].unsqueeze(1).to_broadcast([P, HS, PACK]),
-                    op=ALU.add,
-                )
-            vm_codes = head.tile([P, CHUNKS, HS], U32, tag="vm_codes", align_bytes=64)
-            vm_scales = head.tile([P, CHUNKS, HS], U8, tag="vm_scales", align_bytes=64)
-            nc.vector.quantize_mx(
-                out=vm_codes[:].rearrange("p c d -> p (c d)").bitcast(FP8X4),
-                scales=vm_scales[:].rearrange("p c d -> p (c d)"),
-                in_=vm_grouped[:].rearrange("p c d t -> p (c d t)"),
-            )
-            return vm_codes, vm_scales
+            return v_grouped
 
-        def attend(qT, kT, vm_codes, vm_scales, n, y_ps, row_sums):
-            j = n % Y_GROUP
-            s_ps = []
-            half_max = work.tile([P, CHUNKS], F32, tag="half_max")
-            for g in range(CHUNKS):
-                s_g = psum.tile([P, K_PASS], F32, tag="s", bufs=4, name="s_g")
-                nc.tensor.matmul(
-                    out=s_g[:],
-                    lhsT=qT[:, n * P : (n + 1) * P],
-                    rhs=kT[:, g * K_PASS : (g + 1) * K_PASS],
+        def quantise_pair(grouped, tag):
+            codes = head.tile([P, CHUNKS, HS], U32, tag=tag + "_codes", name="codes", align_bytes=64)
+            scales = head.tile([P, CHUNKS, HS], U8, tag=tag + "_scales", name="scales", align_bytes=64)
+            nc.vector.quantize_mx(
+                out=codes[:].rearrange("p c d -> p (c d)").bitcast(FP8X4),
+                scales=scales[:].rearrange("p c d -> p (c d)"),
+                in_=grouped[:].rearrange("p c d j -> p (c d j)"),
+            )
+            return codes, scales
+
+        def mix_chunk(h, c):
+            codes, scales = v_mx[h]
+            prep_ps[0] = psum.tile([P, PACK, HS], F32, tag="prep", name="vm_ps")
+            for t in range(PACK):
+                m_cols = slice(t * P, (t + 1) * P)
+                nc.tensor.matmul_mx(
+                    out=prep_ps[0][:, t, :],
+                    lhsT=w_words[:, c, m_cols].bitcast(FP8X4),
+                    lhsT_scale=w_scales[:, c, m_cols],
+                    rhs=codes[:, c, :].bitcast(FP8X4),
+                    rhs_scale=scales[:, c, :],
                     start=True,
                     stop=True,
                 )
-                nc.vector.tensor_reduce(out=half_max[:, g : g + 1], in_=s_g[:], axis=AXIS_X, op=ALU.max)
-                s_ps.append(s_g)
-            shift = work.tile([P, 1], F32, tag="shift")
+
+        def add_bias(h, c):
+            nc.vector.tensor_tensor(
+                out=vm_grouped[h][:, c, :, :],
+                in0=prep_ps[0][:].rearrange("p t d -> p d t"),
+                in1=bias[:, c * PACK : (c + 1) * PACK].unsqueeze(1).to_broadcast([P, HS, PACK]),
+                op=ALU.add,
+            )
+
+        def prepare(h, piece):
+            if piece == 0:
+                transpose_tokens(k_sb[h])
+                v_mx[h] = quantise_v(h)
+            if piece == 1:
+                keep_transposed(kT, h, "kT")
+            if piece == 2:
+                transpose_tokens(q_sb[h])
+            if piece == 3:
+                keep_transposed(qT, h, "qT")
+                v_mx[h] = quantise_pair(v_mx[h], "v")
+            if piece == 4:
+                mix_chunk(h, 0)
+            if piece == 5:
+                vm_grouped[h] = head.tile(
+                    [P, CHUNKS, HS, PACK], BF16, tag="vm_grouped", name="vm_grouped", align_bytes=64
+                )
+                add_bias(h, 0)
+            if piece == 6:
+                mix_chunk(h, 1)
+            if piece == 7:
+                add_bias(h, 1)
+                vm_mx[h] = quantise_pair(vm_grouped[h], "vm")
+
+        s_ps, shift, e_sb, eT_ps, e_grouped, e_mx, y_ps, row_sums = {}, {}, {}, {}, {}, {}, {}, {}
+
+        def scores(u):
+            h, n = divmod(u, Q_TILES)
+            half_max = work.tile([P, CHUNKS], F32, tag="half_max")
+            for g in range(CHUNKS):
+                s_ps[u, g] = psum.tile([P, K_PASS], F32, tag="s", bufs=4, name="s_ps")
+                nc.tensor.matmul(
+                    out=s_ps[u, g][:],
+                    lhsT=qT[h][:, n * P : (n + 1) * P],
+                    rhs=kT[h][:, g * K_PASS : (g + 1) * K_PASS],
+                    start=True,
+                    stop=True,
+                )
+                nc.vector.tensor_reduce(
+                    out=half_max[:, g : g + 1], in_=s_ps[u, g][:], axis=AXIS_X, op=ALU.max
+                )
+            shift[u] = work.tile([P, 1], F32, tag="shift", name="shift")
             nc.vector.tensor_scalar(
-                out=shift[:],
+                out=shift[u][:],
                 in0=half_max[:, 0:1],
                 scalar1=half_max[:, 1:2],
                 scalar2=-SCALE,
                 op0=ALU.max,
                 op1=ALU.mult,
             )
-            e_sb = work.tile([P, T], BF16, tag="e_sb")
+
+        def exponentials(u):
+            group, j = divmod(u, Y_GROUP)
+            if j == 0:
+                row_sums[group] = work.tile([P, Y_GROUP, CHUNKS], F32, tag="row_sums", name="row_sums")
+            e_sb[u] = work.tile([P, T], BF16, tag="e_sb", name="e_sb")
             for g in range(CHUNKS):
                 nc.scalar.activation(
-                    out=e_sb[:, g * K_PASS : (g + 1) * K_PASS].rearrange(
+                    out=e_sb[u][:, g * K_PASS : (g + 1) * K_PASS].rearrange(
                         "q (u p e) -> q u p e", u=2, e=2
                     ),
-                    in_=s_ps[g][:].rearrange("q (u e p) -> q u p e", u=2, e=2),
+                    in_=s_ps[u, g][:].rearrange("q (u e p) -> q u p e", u=2, e=2),
                     func=ACT.Exp,
-                    bias=shift[:, 0:1],
+                    bias=shift[u][:, 0:1],
                     scale=SCALE,
-                    accum_out=row_sums[:, j, g : g + 1],
+                    accum_out=row_sums[group][:, j, g : g + 1],
                 )
-            eT_ps = psum.tile([P, 2 * CHUNKS, P], F32, tag="eT", bufs=2)
-            e_words = e_sb[:].bitcast(F32)
+
+        def transpose_e(u):
+            eT_ps[u] = psum.tile([P, 2 * CHUNKS, P], F32, tag="eT", bufs=2, name="eT_ps")
+            e_words = e_sb[u][:].bitcast(F32)
             for w in range(2 * CHUNKS):
                 nc.tensor.transpose(
-                    out=eT_ps[:, w, :], in_=e_words[:, w * P : (w + 1) * P], identity=ident_f32[:]
+                    out=eT_ps[u][:, w, :], in_=e_words[:, w * P : (w + 1) * P], identity=ident_f32[:]
                 )
-            e_grouped = work.tile([P, T], BF16, tag="e_grouped", align_bytes=64)
+
+        def regroup_e(u):
+            e_grouped[u] = work.tile([P, T], BF16, tag="e_grouped", name="e_grouped", align_bytes=64)
             nc.scalar.copy(
-                out=e_grouped[:].bitcast(F32).rearrange("p (g q u) -> p g q u", g=CHUNKS, u=2),
-                in_=eT_ps[:].rearrange("p (g u) q -> p g q u", u=2),
+                out=e_grouped[u][:].bitcast(F32).rearrange("p (g q u) -> p g q u", g=CHUNKS, u=2),
+                in_=eT_ps[u][:].rearrange("p (g u) q -> p g q u", u=2),
             )
-            e_codes = work.tile([P, CHUNKS * P], U32, tag="e_codes", align_bytes=64)
-            e_scales = work.tile([P, CHUNKS * P], U8, tag="e_scales", align_bytes=64)
-            nc.vector.quantize_mx(out=e_codes[:].bitcast(FP8X4), scales=e_scales[:], in_=e_grouped[:])
+
+        def quantise_e(u):
+            codes = work.tile([P, CHUNKS * P], U32, tag="e_codes", align_bytes=64)
+            scales = work.tile([P, CHUNKS * P], U8, tag="e_scales", align_bytes=64)
+            nc.vector.quantize_mx(out=codes[:].bitcast(FP8X4), scales=scales[:], in_=e_grouped[u][:])
+            e_mx[u] = (codes, scales)
+
+        def weighted_values(u):
+            h, n = divmod(u, Q_TILES)
+            group, j = divmod(u, Y_GROUP)
+            if j == 0:
+                y_ps[group] = psum.tile([P, Y_GROUP, HS], F32, tag="y", name="y_ps")
+            codes, scales = e_mx[u]
+            vm_codes, vm_scales = vm_mx[h]
             for g in range(CHUNKS):
                 q_cols = slice(g * P, (g + 1) * P)
                 nc.tensor.matmul_mx(
-                    out=y_ps[:, j, :],
-                    lhsT=e_codes[:, q_cols].bitcast(FP8X4),
-                    lhsT_scale=e_scales[:, q_cols],
+                    out=y_ps[group][:, j, :],
+                    lhsT=codes[:, q_cols].bitcast(FP8X4),
+                    lhsT_scale=scales[:, q_cols],
                     rhs=vm_codes[:, g, :].bitcast(FP8X4),
                     rhs_scale=vm_scales[:, g, :],
                     start=(g == 0),
                     stop=(g == CHUNKS - 1),
                 )
+            if j == Y_GROUP - 1:
+                normalise_and_store(h, n - j, group)
 
-        def normalise_and_store(h, first_n, y_ps, row_sums):
+        def normalise_and_store(h, first_n, group):
             bi, hi = divmod(h, NH)
             row_sum = work.tile([P, Y_GROUP], F32, tag="row_sum")
-            nc.vector.tensor_reduce(out=row_sum[:], in_=row_sums[:], axis=AXIS_X, op=ALU.add)
+            nc.vector.tensor_reduce(out=row_sum[:], in_=row_sums[group][:], axis=AXIS_X, op=ALU.add)
             inv_sum = work.tile([P, Y_GROUP], F32, tag="inv_sum")
             nc.vector.reciprocal(out=inv_sum[:], in_=row_sum[:])
             y_sb = work.tile([P, Y_GROUP, HS], F32, tag="y_sb")
             nc.vector.tensor_tensor(
                 out=y_sb[:],
-                in0=y_ps[:],
+                in0=y_ps[group][:],
                 in1=inv_sum[:].unsqueeze(2).to_broadcast([P, Y_GROUP, HS]),
                 op=ALU.mult,
             )
@@ -225,19 +269,28 @@ def tile_causalselfattention_pb_t_e_kernel(
                 in_=y_sb[:],
             )
 
-        qk = prepare_qk(0)
-        vm = prepare_vm(0)
-        for h in range(HEADS):
-            next_qk, next_vm = None, None
-            for n in range(Q_TILES):
-                if n % Y_GROUP == 0:
-                    y_ps = psum.tile([P, Y_GROUP, HS], F32, tag="y")
-                    row_sums = work.tile([P, Y_GROUP, CHUNKS], F32, tag="row_sums")
-                attend(qk[0], qk[1], vm[0], vm[1], n, y_ps, row_sums)
-                if n % Y_GROUP == Y_GROUP - 1:
-                    normalise_and_store(h, n - (Y_GROUP - 1), y_ps, row_sums)
-                if h + 1 < HEADS and n == 2:
-                    next_qk = prepare_qk(h + 1)
-                if h + 1 < HEADS and n == 5:
-                    next_vm = prepare_vm(h + 1)
-            qk, vm = next_qk, next_vm
+        for piece in range(4):
+            prepare(0, piece)
+        b_ps = psum.tile([P, T], BF16, tag="prep")
+        nc.tensor.transpose(out=b_ps[:, 0:P], in_=b_rows[:], identity=ident_bf[:])
+        bias = const.tile([P, CHUNKS * PACK], F32)
+        nc.vector.tensor_copy(out=bias[:], in_=b_ps[:, 0 : CHUNKS * PACK])
+        scores(0)
+        for piece in range(4, 8):
+            prepare(0, piece)
+
+        for s in range(UNITS + 3):
+            if s + 1 < UNITS:
+                scores(s + 1)
+            if s < UNITS:
+                exponentials(s)
+            if 0 <= s - 1 < UNITS:
+                transpose_e(s - 1)
+                regroup_e(s - 1)
+            if 0 <= s - 2 < UNITS:
+                quantise_e(s - 2)
+            if 0 <= s - 3:
+                weighted_values(s - 3)
+            h, piece = divmod(s, Q_TILES)
+            if h + 1 < HEADS:
+                prepare(h + 1, piece)

@@ -36,7 +36,7 @@ def tile_causalselfattention_pb_t_e_kernel(
         const = stack.enter_context(tc.tile_pool(name="const", bufs=1))
         inputs = stack.enter_context(tc.tile_pool(name="inputs", bufs=1))
         head = stack.enter_context(tc.tile_pool(name="head", bufs=2))
-        work = stack.enter_context(tc.tile_pool(name="work", bufs=3))
+        work = stack.enter_context(tc.tile_pool(name="work", bufs=4))
         psum = stack.enter_context(tc.psum_pool(name="psum", bufs=1))
         stack.enter_context(tc.manual_schedule())
 
@@ -81,7 +81,7 @@ def tile_causalselfattention_pb_t_e_kernel(
         for h in range(1, HEADS):
             load_head(h)
 
-        prep_ps, qT, kT, v_mx, vm_grouped, vm_mx = {}, {}, {}, {}, {}, {}
+        prep_ps, qT, kT, v_grouped, v_mx, vm_grouped, vm_mx = {}, {}, {}, {}, {}, {}, {}
 
         def transpose_tokens(src):
             prep_ps[0] = psum.tile([P, T], BF16, tag="prep", name="tokens_ps")
@@ -92,19 +92,17 @@ def tile_causalselfattention_pb_t_e_kernel(
 
         def keep_transposed(dest, h, tag):
             dest[h] = head.tile([P, T], BF16, tag=tag, name=tag)
-            nc.scalar.copy(out=dest[h][:], in_=prep_ps[0][:])
+            nc.vector.tensor_copy(out=dest[h][:], in_=prep_ps[0][:])
 
-        def quantise_v(h):
-            v_grouped = head.tile([P, CHUNKS, HS, PACK], BF16, tag="v_grouped", align_bytes=64)
+        def regroup_v(h, c):
             nc.gpsimd.tensor_scalar(
-                out=v_grouped[:],
-                in0=v_sb[h][:].rearrange("p c j d -> p c d j"),
+                out=v_grouped[h][:, c, :, :],
+                in0=v_sb[h][:, c, :, :].rearrange("p j d -> p d j"),
                 scalar1=1.0,
                 scalar2=0.0,
                 op0=ALU.mult,
                 op1=ALU.add,
             )
-            return v_grouped
 
         def quantise_pair(grouped, tag):
             codes = head.tile([P, CHUNKS, HS], U32, tag=tag + "_codes", name="codes", align_bytes=64)
@@ -142,14 +140,18 @@ def tile_causalselfattention_pb_t_e_kernel(
         def prepare(h, piece):
             if piece == 0:
                 transpose_tokens(k_sb[h])
-                v_mx[h] = quantise_v(h)
+                v_grouped[h] = head.tile(
+                    [P, CHUNKS, HS, PACK], BF16, tag="v_grouped", name="v_grouped", align_bytes=64
+                )
+                regroup_v(h, 0)
             if piece == 1:
                 keep_transposed(kT, h, "kT")
+                regroup_v(h, 1)
             if piece == 2:
                 transpose_tokens(q_sb[h])
             if piece == 3:
                 keep_transposed(qT, h, "qT")
-                v_mx[h] = quantise_pair(v_mx[h], "v")
+                v_mx[h] = quantise_pair(v_grouped[h], "v")
             if piece == 4:
                 mix_chunk(h, 0)
             if piece == 5:
@@ -181,7 +183,7 @@ def tile_causalselfattention_pb_t_e_kernel(
                     out=half_max[:, g : g + 1], in_=s_ps[u, g][:], axis=AXIS_X, op=ALU.max
                 )
             shift[u] = work.tile([P, 1], F32, tag="shift", name="shift")
-            nc.vector.tensor_scalar(
+            nc.gpsimd.tensor_scalar(
                 out=shift[u][:],
                 in0=half_max[:, 0:1],
                 scalar1=half_max[:, 1:2],
@@ -252,7 +254,9 @@ def tile_causalselfattention_pb_t_e_kernel(
         def normalise_and_store(h, first_n, group):
             bi, hi = divmod(h, NH)
             row_sum = work.tile([P, Y_GROUP], F32, tag="row_sum")
-            nc.vector.tensor_reduce(out=row_sum[:], in_=row_sums[group][:], axis=AXIS_X, op=ALU.add)
+            nc.gpsimd.tensor_tensor(
+                out=row_sum[:], in0=row_sums[group][:, :, 0], in1=row_sums[group][:, :, 1], op=ALU.add
+            )
             inv_sum = work.tile([P, Y_GROUP], F32, tag="inv_sum")
             nc.vector.reciprocal(out=inv_sum[:], in_=row_sum[:])
             y_sb = work.tile([P, Y_GROUP, HS], F32, tag="y_sb")
@@ -279,7 +283,9 @@ def tile_causalselfattention_pb_t_e_kernel(
         for piece in range(4, 8):
             prepare(0, piece)
 
-        for s in range(UNITS + 3):
+        for s in range(UNITS + 4):
+            if 0 <= s - 3 < UNITS:
+                quantise_e(s - 3)
             if s + 1 < UNITS:
                 scores(s + 1)
             if s < UNITS:
@@ -287,10 +293,8 @@ def tile_causalselfattention_pb_t_e_kernel(
             if 0 <= s - 1 < UNITS:
                 transpose_e(s - 1)
                 regroup_e(s - 1)
-            if 0 <= s - 2 < UNITS:
-                quantise_e(s - 2)
-            if 0 <= s - 3:
-                weighted_values(s - 3)
+            if 0 <= s - 4:
+                weighted_values(s - 4)
             h, piece = divmod(s, Q_TILES)
             if h + 1 < HEADS:
                 prepare(h + 1, piece)

@@ -36,7 +36,7 @@ def tile_causalselfattention_pb_t_e_kernel(
         const = stack.enter_context(tc.tile_pool(name="const", bufs=1))
         inputs = stack.enter_context(tc.tile_pool(name="inputs", bufs=1))
         head = stack.enter_context(tc.tile_pool(name="head", bufs=2))
-        work = stack.enter_context(tc.tile_pool(name="work", bufs=4))
+        work = stack.enter_context(tc.tile_pool(name="work", bufs=3))
         psum = stack.enter_context(tc.psum_pool(name="psum", bufs=1))
         stack.enter_context(tc.manual_schedule())
 
@@ -81,7 +81,7 @@ def tile_causalselfattention_pb_t_e_kernel(
         for h in range(1, HEADS):
             load_head(h)
 
-        prep_ps, qT, kT, v_grouped, v_mx, vm_grouped, vm_mx = {}, {}, {}, {}, {}, {}, {}
+        prep_ps, qT, kT, v_mx, vm_grouped, vm_mx = {}, {}, {}, {}, {}, {}
 
         def transpose_tokens(src):
             prep_ps[0] = psum.tile([P, T], BF16, tag="prep", name="tokens_ps")
@@ -92,17 +92,19 @@ def tile_causalselfattention_pb_t_e_kernel(
 
         def keep_transposed(dest, h, tag):
             dest[h] = head.tile([P, T], BF16, tag=tag, name=tag)
-            nc.vector.tensor_copy(out=dest[h][:], in_=prep_ps[0][:])
+            nc.scalar.copy(out=dest[h][:].bitcast(F32), in_=prep_ps[0][:].bitcast(F32))
 
-        def regroup_v(h, c):
+        def quantise_v(h):
+            v_grouped = head.tile([P, CHUNKS, HS, PACK], BF16, tag="v_grouped", align_bytes=64)
             nc.gpsimd.tensor_scalar(
-                out=v_grouped[h][:, c, :, :],
-                in0=v_sb[h][:, c, :, :].rearrange("p j d -> p d j"),
+                out=v_grouped[:],
+                in0=v_sb[h][:].rearrange("p c j d -> p c d j"),
                 scalar1=1.0,
                 scalar2=0.0,
                 op0=ALU.mult,
                 op1=ALU.add,
             )
+            return v_grouped
 
         def quantise_pair(grouped, tag):
             codes = head.tile([P, CHUNKS, HS], U32, tag=tag + "_codes", name="codes", align_bytes=64)
@@ -140,18 +142,14 @@ def tile_causalselfattention_pb_t_e_kernel(
         def prepare(h, piece):
             if piece == 0:
                 transpose_tokens(k_sb[h])
-                v_grouped[h] = head.tile(
-                    [P, CHUNKS, HS, PACK], BF16, tag="v_grouped", name="v_grouped", align_bytes=64
-                )
-                regroup_v(h, 0)
+                v_mx[h] = quantise_v(h)
             if piece == 1:
                 keep_transposed(kT, h, "kT")
-                regroup_v(h, 1)
             if piece == 2:
                 transpose_tokens(q_sb[h])
             if piece == 3:
                 keep_transposed(qT, h, "qT")
-                v_mx[h] = quantise_pair(v_grouped[h], "v")
+                v_mx[h] = quantise_pair(v_mx[h], "v")
             if piece == 4:
                 mix_chunk(h, 0)
             if piece == 5:
@@ -163,13 +161,15 @@ def tile_causalselfattention_pb_t_e_kernel(
                 mix_chunk(h, 1)
             if piece == 7:
                 add_bias(h, 1)
+            if piece == 8:
                 vm_mx[h] = quantise_pair(vm_grouped[h], "vm")
 
-        s_ps, shift, e_sb, eT_ps, e_grouped, e_mx, y_ps, row_sums = {}, {}, {}, {}, {}, {}, {}, {}
+        s_ps, half_max, shift, e_sb, eT_ps, e_grouped, e_mx = {}, {}, {}, {}, {}, {}, {}
+        y_ps, row_sums, row_sum, inv_sum = {}, {}, {}, {}
 
         def scores(u):
             h, n = divmod(u, Q_TILES)
-            half_max = work.tile([P, CHUNKS], F32, tag="half_max")
+            half_max[u] = work.tile([P, CHUNKS], F32, tag="half_max", name="half_max")
             for g in range(CHUNKS):
                 s_ps[u, g] = psum.tile([P, K_PASS], F32, tag="s", bufs=4, name="s_ps")
                 nc.tensor.matmul(
@@ -180,13 +180,15 @@ def tile_causalselfattention_pb_t_e_kernel(
                     stop=True,
                 )
                 nc.vector.tensor_reduce(
-                    out=half_max[:, g : g + 1], in_=s_ps[u, g][:], axis=AXIS_X, op=ALU.max
+                    out=half_max[u][:, g : g + 1], in_=s_ps[u, g][:], axis=AXIS_X, op=ALU.max
                 )
+
+        def row_shift(u):
             shift[u] = work.tile([P, 1], F32, tag="shift", name="shift")
-            nc.gpsimd.tensor_scalar(
+            nc.vector.tensor_scalar(
                 out=shift[u][:],
-                in0=half_max[:, 0:1],
-                scalar1=half_max[:, 1:2],
+                in0=half_max[u][:, 0:1],
+                scalar1=half_max[u][:, 1:2],
                 scalar2=-SCALE,
                 op0=ALU.max,
                 op1=ALU.mult,
@@ -248,22 +250,26 @@ def tile_causalselfattention_pb_t_e_kernel(
                     start=(g == 0),
                     stop=(g == CHUNKS - 1),
                 )
-            if j == Y_GROUP - 1:
-                normalise_and_store(h, n - j, group)
 
-        def normalise_and_store(h, first_n, group):
-            bi, hi = divmod(h, NH)
-            row_sum = work.tile([P, Y_GROUP], F32, tag="row_sum")
-            nc.gpsimd.tensor_tensor(
-                out=row_sum[:], in0=row_sums[group][:, :, 0], in1=row_sums[group][:, :, 1], op=ALU.add
+        def add_row_sums(group):
+            row_sum[group] = work.tile([P, Y_GROUP], F32, tag="row_sum", name="row_sum")
+            nc.vector.tensor_reduce(
+                out=row_sum[group][:], in_=row_sums[group][:], axis=AXIS_X, op=ALU.add
             )
-            inv_sum = work.tile([P, Y_GROUP], F32, tag="inv_sum")
-            nc.vector.reciprocal(out=inv_sum[:], in_=row_sum[:])
+
+        def invert_row_sums(group):
+            inv_sum[group] = work.tile([P, Y_GROUP], F32, tag="inv_sum", name="inv_sum")
+            nc.vector.reciprocal(out=inv_sum[group][:], in_=row_sum[group][:])
+
+        def normalise_and_store(group):
+            h, half = divmod(group, Q_TILES // Y_GROUP)
+            first_n = half * Y_GROUP
+            bi, hi = divmod(h, NH)
             y_sb = work.tile([P, Y_GROUP, HS], F32, tag="y_sb")
             nc.vector.tensor_tensor(
                 out=y_sb[:],
                 in0=y_ps[group][:],
-                in1=inv_sum[:].unsqueeze(2).to_broadcast([P, Y_GROUP, HS]),
+                in1=inv_sum[group][:].unsqueeze(2).to_broadcast([P, Y_GROUP, HS]),
                 op=ALU.mult,
             )
             nc.sync.dma_start(
@@ -280,21 +286,35 @@ def tile_causalselfattention_pb_t_e_kernel(
         bias = const.tile([P, CHUNKS * PACK], F32)
         nc.vector.tensor_copy(out=bias[:], in_=b_ps[:, 0 : CHUNKS * PACK])
         scores(0)
-        for piece in range(4, 8):
+        for piece in range(4, 9):
             prepare(0, piece)
+        row_shift(0)
 
-        for s in range(UNITS + 4):
-            if 0 <= s - 3 < UNITS:
-                quantise_e(s - 3)
+        def ends_group(u):
+            return 0 <= u < UNITS and u % Y_GROUP == Y_GROUP - 1
+
+        for s in range(UNITS + 3):
             if s + 1 < UNITS:
                 scores(s + 1)
+            if 0 <= s - 2 < UNITS:
+                quantise_e(s - 2)
+            if s + 1 < UNITS:
+                row_shift(s + 1)
             if s < UNITS:
                 exponentials(s)
             if 0 <= s - 1 < UNITS:
                 transpose_e(s - 1)
                 regroup_e(s - 1)
-            if 0 <= s - 4:
-                weighted_values(s - 4)
+            if 0 <= s - 3:
+                weighted_values(s - 3)
+            if ends_group(s - 1):
+                add_row_sums((s - 1) // Y_GROUP)
+            if ends_group(s - 2):
+                invert_row_sums((s - 2) // Y_GROUP)
+            if ends_group(s - 3):
+                normalise_and_store((s - 3) // Y_GROUP)
             h, piece = divmod(s, Q_TILES)
+            if piece == 0 and 1 <= h < HEADS:
+                prepare(h, Q_TILES)
             if h + 1 < HEADS:
                 prepare(h + 1, piece)

@@ -90,9 +90,9 @@ def tile_causalselfattention_pb_t_e_kernel(
                     out=prep_ps[0][:, n * P : (n + 1) * P], in_=src[:, n, :], identity=ident_bf[:]
                 )
 
-        def keep_transposed(dest, h, tag):
+        def keep_transposed(copy, dest, h, tag):
             dest[h] = head.tile([P, T], BF16, tag=tag, name=tag)
-            nc.scalar.copy(out=dest[h][:].bitcast(F32), in_=prep_ps[0][:].bitcast(F32))
+            copy(out=dest[h][:].bitcast(F32), in_=prep_ps[0][:].bitcast(F32))
 
         def quantise_v(h):
             v_grouped = head.tile([P, CHUNKS, HS, PACK], BF16, tag="v_grouped", align_bytes=64)
@@ -144,12 +144,12 @@ def tile_causalselfattention_pb_t_e_kernel(
                 transpose_tokens(k_sb[h])
                 v_mx[h] = quantise_v(h)
             if piece == 1:
-                keep_transposed(kT, h, "kT")
+                keep_transposed(nc.scalar.copy, kT, h, "kT")
+                v_mx[h] = quantise_pair(v_mx[h], "v")
             if piece == 2:
                 transpose_tokens(q_sb[h])
             if piece == 3:
-                keep_transposed(qT, h, "qT")
-                v_mx[h] = quantise_pair(v_mx[h], "v")
+                keep_transposed(nc.vector.tensor_copy, qT, h, "qT")
             if piece == 4:
                 mix_chunk(h, 0)
             if piece == 5:

@@ -21,9 +21,13 @@ B, NH, T, HS = 4, 4, 1024, 128
 HEADS = B * NH
 CHUNKS = T // K_PASS
 Q_TILES = T // P
-Y_GROUP = 4
 UNITS = HEADS * Q_TILES
+Y_GROUP = 4
 SCALE = 1.0 / math.sqrt(HS)
+
+HEAD_BUFS = 2
+WORK_BUFS = 3
+ROTATING_BANKS = 7
 
 FLOPS = 2 * HEADS * (T * K_PASS * HS + 2 * T * T * HS)
 
@@ -35,10 +39,13 @@ def tile_causalselfattention_pb_t_e_kernel(
     with ExitStack() as stack:
         const = stack.enter_context(tc.tile_pool(name="const", bufs=1))
         inputs = stack.enter_context(tc.tile_pool(name="inputs", bufs=1))
-        head = stack.enter_context(tc.tile_pool(name="head", bufs=2))
-        work = stack.enter_context(tc.tile_pool(name="work", bufs=3))
+        head = stack.enter_context(tc.tile_pool(name="head", bufs=HEAD_BUFS))
+        work = stack.enter_context(tc.tile_pool(name="work", bufs=WORK_BUFS))
         psum = stack.enter_context(tc.psum_pool(name="psum", bufs=1))
         stack.enter_context(tc.manual_schedule())
+
+        def bank(shape, dtype, name):
+            return psum.tile(shape, dtype, tag="bank", bufs=ROTATING_BANKS, name=name)
 
         k_sb, q_sb, v_sb = {}, {}, {}
 
@@ -81,32 +88,33 @@ def tile_causalselfattention_pb_t_e_kernel(
         for h in range(1, HEADS):
             load_head(h)
 
-        prep_ps, qT, kT, v_mx, vm_grouped, vm_mx = {}, {}, {}, {}, {}, {}
+        tokens_ps, vm_ps, qT, kT, v_grouped, v_mx, vm_grouped, vm_mx = {}, {}, {}, {}, {}, {}, {}, {}
 
-        def transpose_tokens(src):
-            prep_ps[0] = psum.tile([P, T], BF16, tag="prep", name="tokens_ps")
+        def transpose_tokens(src, h):
+            tokens_ps[h] = bank([P, T], BF16, "tokens_ps")
             for n in range(Q_TILES):
                 nc.tensor.transpose(
-                    out=prep_ps[0][:, n * P : (n + 1) * P], in_=src[:, n, :], identity=ident_bf[:]
+                    out=tokens_ps[h][:, n * P : (n + 1) * P], in_=src[:, n, :], identity=ident_bf[:]
                 )
 
-        def keep_transposed(copy, dest, h, tag):
+        def keep_transposed(dest, h, tag):
             dest[h] = head.tile([P, T], BF16, tag=tag, name=tag)
-            copy(out=dest[h][:].bitcast(F32), in_=prep_ps[0][:].bitcast(F32))
+            nc.scalar.copy(out=dest[h][:].bitcast(F32), in_=tokens_ps[h][:].bitcast(F32))
 
-        def quantise_v(h):
-            v_grouped = head.tile([P, CHUNKS, HS, PACK], BF16, tag="v_grouped", align_bytes=64)
+        def regroup_v(h):
+            v_grouped[h] = head.tile(
+                [P, CHUNKS, HS, PACK], BF16, tag="v_grouped", name="v_grouped", align_bytes=64
+            )
             nc.gpsimd.tensor_scalar(
-                out=v_grouped[:],
+                out=v_grouped[h][:],
                 in0=v_sb[h][:].rearrange("p c j d -> p c d j"),
                 scalar1=1.0,
                 scalar2=0.0,
                 op0=ALU.mult,
                 op1=ALU.add,
             )
-            return v_grouped
 
-        def quantise_pair(grouped, tag):
+        def quantise_values(grouped, tag):
             codes = head.tile([P, CHUNKS, HS], U32, tag=tag + "_codes", name="codes", align_bytes=64)
             scales = head.tile([P, CHUNKS, HS], U8, tag=tag + "_scales", name="scales", align_bytes=64)
             nc.vector.quantize_mx(
@@ -118,11 +126,11 @@ def tile_causalselfattention_pb_t_e_kernel(
 
         def mix_chunk(h, c):
             codes, scales = v_mx[h]
-            prep_ps[0] = psum.tile([P, PACK, HS], F32, tag="prep", name="vm_ps")
+            vm_ps[h] = bank([P, PACK, HS], F32, "vm_ps")
             for t in range(PACK):
                 m_cols = slice(t * P, (t + 1) * P)
                 nc.tensor.matmul_mx(
-                    out=prep_ps[0][:, t, :],
+                    out=vm_ps[h][:, t, :],
                     lhsT=w_words[:, c, m_cols].bitcast(FP8X4),
                     lhsT_scale=w_scales[:, c, m_cols],
                     rhs=codes[:, c, :].bitcast(FP8X4),
@@ -134,22 +142,22 @@ def tile_causalselfattention_pb_t_e_kernel(
         def add_bias(h, c):
             nc.vector.tensor_tensor(
                 out=vm_grouped[h][:, c, :, :],
-                in0=prep_ps[0][:].rearrange("p t d -> p d t"),
+                in0=vm_ps[h][:].rearrange("p t d -> p d t"),
                 in1=bias[:, c * PACK : (c + 1) * PACK].unsqueeze(1).to_broadcast([P, HS, PACK]),
                 op=ALU.add,
             )
 
         def prepare(h, piece):
             if piece == 0:
-                transpose_tokens(k_sb[h])
-                v_mx[h] = quantise_v(h)
+                transpose_tokens(k_sb[h], h)
+                regroup_v(h)
             if piece == 1:
-                keep_transposed(nc.scalar.copy, kT, h, "kT")
-                v_mx[h] = quantise_pair(v_mx[h], "v")
+                keep_transposed(kT, h, "kT")
             if piece == 2:
-                transpose_tokens(q_sb[h])
+                transpose_tokens(q_sb[h], h)
             if piece == 3:
-                keep_transposed(nc.vector.tensor_copy, qT, h, "qT")
+                keep_transposed(qT, h, "qT")
+                v_mx[h] = quantise_values(v_grouped[h], "v")
             if piece == 4:
                 mix_chunk(h, 0)
             if piece == 5:
@@ -162,16 +170,15 @@ def tile_causalselfattention_pb_t_e_kernel(
             if piece == 7:
                 add_bias(h, 1)
             if piece == 8:
-                vm_mx[h] = quantise_pair(vm_grouped[h], "vm")
+                vm_mx[h] = quantise_values(vm_grouped[h], "vm")
 
         s_ps, half_max, shift, e_sb, eT_ps, e_grouped, e_mx = {}, {}, {}, {}, {}, {}, {}
-        y_ps, row_sums, row_sum, inv_sum = {}, {}, {}, {}
 
         def scores(u):
             h, n = divmod(u, Q_TILES)
             half_max[u] = work.tile([P, CHUNKS], F32, tag="half_max", name="half_max")
             for g in range(CHUNKS):
-                s_ps[u, g] = psum.tile([P, K_PASS], F32, tag="s", bufs=4, name="s_ps")
+                s_ps[u, g] = bank([P, K_PASS], F32, "s_ps")
                 nc.tensor.matmul(
                     out=s_ps[u, g][:],
                     lhsT=qT[h][:, n * P : (n + 1) * P],
@@ -202,9 +209,9 @@ def tile_causalselfattention_pb_t_e_kernel(
             for g in range(CHUNKS):
                 nc.scalar.activation(
                     out=e_sb[u][:, g * K_PASS : (g + 1) * K_PASS].rearrange(
-                        "q (u p e) -> q u p e", u=2, e=2
+                        "q (w p e) -> q w p e", p=P, e=2
                     ),
-                    in_=s_ps[u, g][:].rearrange("q (u e p) -> q u p e", u=2, e=2),
+                    in_=s_ps[u, g][:].rearrange("q (w e p) -> q w p e", p=P, e=2),
                     func=ACT.Exp,
                     bias=shift[u][:, 0:1],
                     scale=SCALE,
@@ -212,7 +219,7 @@ def tile_causalselfattention_pb_t_e_kernel(
                 )
 
         def transpose_e(u):
-            eT_ps[u] = psum.tile([P, 2 * CHUNKS, P], F32, tag="eT", bufs=2, name="eT_ps")
+            eT_ps[u] = bank([P, 2 * CHUNKS, P], F32, "eT_ps")
             e_words = e_sb[u][:].bitcast(F32)
             for w in range(2 * CHUNKS):
                 nc.tensor.transpose(
@@ -222,8 +229,8 @@ def tile_causalselfattention_pb_t_e_kernel(
         def regroup_e(u):
             e_grouped[u] = work.tile([P, T], BF16, tag="e_grouped", name="e_grouped", align_bytes=64)
             nc.scalar.copy(
-                out=e_grouped[u][:].bitcast(F32).rearrange("p (g q u) -> p g q u", g=CHUNKS, u=2),
-                in_=eT_ps[u][:].rearrange("p (g u) q -> p g q u", u=2),
+                out=e_grouped[u][:].bitcast(F32).rearrange("p (g q w) -> p g q w", g=CHUNKS, w=2),
+                in_=eT_ps[u][:].rearrange("p (g w) q -> p g q w", w=2),
             )
 
         def quantise_e(u):
@@ -233,12 +240,11 @@ def tile_causalselfattention_pb_t_e_kernel(
             e_mx[u] = (codes, scales)
 
         def weighted_values(u):
-            h, n = divmod(u, Q_TILES)
             group, j = divmod(u, Y_GROUP)
             if j == 0:
                 y_ps[group] = psum.tile([P, Y_GROUP, HS], F32, tag="y", name="y_ps")
             codes, scales = e_mx[u]
-            vm_codes, vm_scales = vm_mx[h]
+            vm_codes, vm_scales = vm_mx[u // Q_TILES]
             for g in range(CHUNKS):
                 q_cols = slice(g * P, (g + 1) * P)
                 nc.tensor.matmul_mx(
@@ -250,6 +256,8 @@ def tile_causalselfattention_pb_t_e_kernel(
                     start=(g == 0),
                     stop=(g == CHUNKS - 1),
                 )
+
+        y_ps, row_sums, row_sum, inv_sum = {}, {}, {}, {}
 
         def add_row_sums(group):
             row_sum[group] = work.tile([P, Y_GROUP], F32, tag="row_sum", name="row_sum")
@@ -281,7 +289,7 @@ def tile_causalselfattention_pb_t_e_kernel(
 
         for piece in range(4):
             prepare(0, piece)
-        b_ps = psum.tile([P, T], BF16, tag="prep")
+        b_ps = bank([P, T], BF16, "b_ps")
         nc.tensor.transpose(out=b_ps[:, 0:P], in_=b_rows[:], identity=ident_bf[:])
         bias = const.tile([P, CHUNKS * PACK], F32)
         nc.vector.tensor_copy(out=bias[:], in_=b_ps[:, 0 : CHUNKS * PACK])
@@ -290,22 +298,25 @@ def tile_causalselfattention_pb_t_e_kernel(
             prepare(0, piece)
         row_shift(0)
 
+        def is_unit(u):
+            return 0 <= u < UNITS
+
         def ends_group(u):
-            return 0 <= u < UNITS and u % Y_GROUP == Y_GROUP - 1
+            return is_unit(u) and u % Y_GROUP == Y_GROUP - 1
 
         for s in range(UNITS + 3):
-            if s + 1 < UNITS:
+            if is_unit(s + 1):
                 scores(s + 1)
-            if 0 <= s - 2 < UNITS:
+            if is_unit(s - 2):
                 quantise_e(s - 2)
-            if s + 1 < UNITS:
+            if is_unit(s + 1):
                 row_shift(s + 1)
-            if s < UNITS:
+            if is_unit(s):
                 exponentials(s)
-            if 0 <= s - 1 < UNITS:
+            if is_unit(s - 1):
                 transpose_e(s - 1)
                 regroup_e(s - 1)
-            if 0 <= s - 3:
+            if is_unit(s - 3):
                 weighted_values(s - 3)
             if ends_group(s - 1):
                 add_row_sums((s - 1) // Y_GROUP)

@@ -25,6 +25,7 @@ UNITS = HEADS * Q_TILES
 Y_GROUP = 4
 SCALE = 1.0 / math.sqrt(HS)
 
+V_PIECES = 8
 HEAD_BUFS = 2
 WORK_BUFS = 3
 ROTATING_BANKS = 7
@@ -101,13 +102,17 @@ def tile_causalselfattention_pb_t_e_kernel(
             dest[h] = head.tile([P, T], BF16, tag=tag, name=tag)
             nc.scalar.copy(out=dest[h][:].bitcast(F32), in_=tokens_ps[h][:].bitcast(F32))
 
-        def regroup_v(h):
-            v_grouped[h] = head.tile(
-                [P, CHUNKS, HS, PACK], BF16, tag="v_grouped", name="v_grouped", align_bytes=64
-            )
+        def regroup_v(h, piece):
+            if piece == 0:
+                v_grouped[h] = head.tile(
+                    [P, CHUNKS, HS, PACK], BF16, tag="v_grouped", name="v_grouped", align_bytes=64
+                )
+            c, part = divmod(piece, V_PIECES // CHUNKS)
+            width = HS * CHUNKS // V_PIECES
+            channels = slice(part * width, (part + 1) * width)
             nc.gpsimd.tensor_scalar(
-                out=v_grouped[h][:],
-                in0=v_sb[h][:].rearrange("p c j d -> p c d j"),
+                out=v_grouped[h][:, c, channels, :],
+                in0=v_sb[h][:, c, :, channels].rearrange("p j d -> p d j"),
                 scalar1=1.0,
                 scalar2=0.0,
                 op0=ALU.mult,
@@ -150,7 +155,6 @@ def tile_causalselfattention_pb_t_e_kernel(
         def prepare(h, piece):
             if piece == 0:
                 transpose_tokens(k_sb[h], h)
-                regroup_v(h)
             if piece == 1:
                 keep_transposed(kT, h, "kT")
             if piece == 2:
@@ -287,6 +291,9 @@ def tile_causalselfattention_pb_t_e_kernel(
                 in_=y_sb[:],
             )
 
+        for h in range(2):
+            for piece in range(V_PIECES):
+                regroup_v(h, piece)
         for piece in range(4):
             prepare(0, piece)
         b_ps = bank([P, T], BF16, "b_ps")
@@ -329,3 +336,5 @@ def tile_causalselfattention_pb_t_e_kernel(
                 prepare(h, Q_TILES)
             if h + 1 < HEADS:
                 prepare(h + 1, piece)
+            if h + 2 < HEADS:
+                regroup_v(h + 2, piece)

@@ -24,6 +24,8 @@ Q_TILES = T // P
 UNITS = HEADS * Q_TILES
 Y_GROUP = 4
 SCALE = 1.0 / math.sqrt(HS)
+ALL_TILES = range(Q_TILES)
+FIRST_HALF, SECOND_HALF = ALL_TILES[: Q_TILES // 2], ALL_TILES[Q_TILES // 2 :]
 
 V_PIECES = 8
 HEAD_BUFS = 2
@@ -53,7 +55,13 @@ def tile_causalselfattention_pb_t_e_kernel(
         def load_head(h):
             bi, hi = divmod(h, NH)
             k_sb[h] = inputs.tile([P, Q_TILES, HS], BF16, name="k_sb%d" % h)
-            nc.sync.dma_start(out=k_sb[h][:], in_=k_mix[bi, hi].rearrange("(n p) d -> p n d", p=P))
+            halves = 2 if h == 0 else 1
+            for i in range(halves):
+                tiles = slice(i * Q_TILES // halves, (i + 1) * Q_TILES // halves)
+                nc.sync.dma_start(
+                    out=k_sb[h][:, tiles, :],
+                    in_=k_mix[bi, hi].rearrange("(n p) d -> p n d", p=P)[:, tiles, :],
+                )
             q_sb[h] = inputs.tile([P, Q_TILES, HS], BF16, name="q_sb%d" % h)
             nc.sync.dma_start(out=q_sb[h][:], in_=q[bi, hi].rearrange("(p n) d -> p n d", n=Q_TILES))
             v_sb[h] = inputs.tile([P, CHUNKS, PACK, HS], BF16, name="v_sb%d" % h)
@@ -89,18 +97,22 @@ def tile_causalselfattention_pb_t_e_kernel(
         for h in range(1, HEADS):
             load_head(h)
 
-        tokens_ps, vm_ps, qT, kT, v_grouped, v_mx, vm_grouped, vm_mx = {}, {}, {}, {}, {}, {}, {}, {}
+        tokens_ps, vm_ps, qT, kT = {}, {}, {}, {}
+        v_grouped, v_mx, vm_grouped, vm_mx = {}, {}, {}, {}
 
-        def transpose_tokens(src, h):
-            tokens_ps[h] = bank([P, T], BF16, "tokens_ps")
-            for n in range(Q_TILES):
+        def transpose_tokens(src, tiles):
+            tokens_ps = bank([P, len(tiles) * P], BF16, "tokens_ps")
+            for i, n in enumerate(tiles):
                 nc.tensor.transpose(
-                    out=tokens_ps[h][:, n * P : (n + 1) * P], in_=src[:, n, :], identity=ident_bf[:]
+                    out=tokens_ps[:, i * P : (i + 1) * P], in_=src[:, n, :], identity=ident_bf[:]
                 )
+            return tokens_ps
 
-        def keep_transposed(dest, h, tag):
-            dest[h] = head.tile([P, T], BF16, tag=tag, name=tag)
-            nc.scalar.copy(out=dest[h][:].bitcast(F32), in_=tokens_ps[h][:].bitcast(F32))
+        def keep_transposed(tokens_ps, dest, tag, h, tiles, copy):
+            if 0 in tiles:
+                dest[h] = head.tile([P, T], BF16, tag=tag, name=tag)
+            cols = slice(tiles[0] * P, (tiles[-1] + 1) * P)
+            copy(out=dest[h][:, cols].bitcast(F32), in_=tokens_ps[:].bitcast(F32))
 
         def regroup_v(h, piece):
             if piece == 0:
@@ -152,28 +164,28 @@ def tile_causalselfattention_pb_t_e_kernel(
                 op=ALU.add,
             )
 
-        def prepare(h, piece):
-            if piece == 0:
-                transpose_tokens(k_sb[h], h)
-            if piece == 1:
-                keep_transposed(kT, h, "kT")
-            if piece == 2:
-                transpose_tokens(q_sb[h], h)
-            if piece == 3:
-                keep_transposed(qT, h, "qT")
+        def prepare(h, when):
+            if when == -8:
+                tokens_ps[h] = transpose_tokens(k_sb[h], ALL_TILES)
+            if when == -7:
+                keep_transposed(tokens_ps[h], kT, "kT", h, ALL_TILES, nc.scalar.copy)
+            if when == -6:
+                tokens_ps[h] = transpose_tokens(q_sb[h], ALL_TILES)
+            if when == -5:
+                keep_transposed(tokens_ps[h], qT, "qT", h, ALL_TILES, nc.scalar.copy)
                 v_mx[h] = quantise_values(v_grouped[h], "v")
-            if piece == 4:
+            if when == -4:
                 mix_chunk(h, 0)
-            if piece == 5:
+            if when == -3:
                 vm_grouped[h] = head.tile(
                     [P, CHUNKS, HS, PACK], BF16, tag="vm_grouped", name="vm_grouped", align_bytes=64
                 )
                 add_bias(h, 0)
-            if piece == 6:
+            if when == -2:
                 mix_chunk(h, 1)
-            if piece == 7:
+            if when == -1:
                 add_bias(h, 1)
-            if piece == 8:
+            if when == 0:
                 vm_mx[h] = quantise_values(vm_grouped[h], "vm")
 
         s_ps, half_max, shift, e_sb, eT_ps, e_grouped, e_mx = {}, {}, {}, {}, {}, {}, {}
@@ -291,19 +303,23 @@ def tile_causalselfattention_pb_t_e_kernel(
                 in_=y_sb[:],
             )
 
-        for h in range(2):
-            for piece in range(V_PIECES):
-                regroup_v(h, piece)
-        for piece in range(4):
-            prepare(0, piece)
+        for piece in range(V_PIECES):
+            regroup_v(0, piece)
+        for tiles, copy in ((FIRST_HALF, nc.scalar.copy), (SECOND_HALF, nc.vector.tensor_copy)):
+            keep_transposed(transpose_tokens(k_sb[0], tiles), kT, "kT", 0, tiles, copy)
+        keep_transposed(transpose_tokens(q_sb[0], FIRST_HALF), qT, "qT", 0, FIRST_HALF, nc.scalar.copy)
+        scores(0)
+        row_shift(0)
+        keep_transposed(transpose_tokens(q_sb[0], SECOND_HALF), qT, "qT", 0, SECOND_HALF, nc.scalar.copy)
         b_ps = bank([P, T], BF16, "b_ps")
         nc.tensor.transpose(out=b_ps[:, 0:P], in_=b_rows[:], identity=ident_bf[:])
         bias = const.tile([P, CHUNKS * PACK], F32)
         nc.vector.tensor_copy(out=bias[:], in_=b_ps[:, 0 : CHUNKS * PACK])
-        scores(0)
-        for piece in range(4, 9):
-            prepare(0, piece)
-        row_shift(0)
+        v_mx[0] = quantise_values(v_grouped[0], "v")
+        for when in range(-4, 0):
+            prepare(0, when)
+        for piece in range(V_PIECES):
+            regroup_v(1, piece)
 
         def is_unit(u):
             return 0 <= u < UNITS
@@ -331,10 +347,10 @@ def tile_causalselfattention_pb_t_e_kernel(
                 invert_row_sums((s - 2) // Y_GROUP)
             if ends_group(s - 3):
                 normalise_and_store((s - 3) // Y_GROUP)
-            h, piece = divmod(s, Q_TILES)
-            if piece == 0 and 1 <= h < HEADS:
-                prepare(h, Q_TILES)
+            h, j = divmod(s, Q_TILES)
+            if h < HEADS:
+                prepare(h, j)
             if h + 1 < HEADS:
-                prepare(h + 1, piece)
+                prepare(h + 1, j - Q_TILES)
             if h + 2 < HEADS:
-                regroup_v(h + 2, piece)
+                regroup_v(h + 2, j)

@@ -28,6 +28,7 @@ ALL_TILES = range(Q_TILES)
 FIRST_HALF, SECOND_HALF = ALL_TILES[: Q_TILES // 2], ALL_TILES[Q_TILES // 2 :]
 
 V_PIECES = 8
+SCALAR_EVERY = 4
 HEAD_BUFS = 2
 WORK_BUFS = 3
 ROTATING_BANKS = 7
@@ -55,19 +56,23 @@ def tile_causalselfattention_pb_t_e_kernel(
         def load_head(h):
             bi, hi = divmod(h, NH)
             k_sb[h] = inputs.tile([P, Q_TILES, HS], BF16, name="k_sb%d" % h)
-            halves = 2 if h == 0 else 1
-            for i in range(halves):
-                tiles = slice(i * Q_TILES // halves, (i + 1) * Q_TILES // halves)
-                nc.sync.dma_start(
-                    out=k_sb[h][:, tiles, :],
-                    in_=k_mix[bi, hi].rearrange("(n p) d -> p n d", p=P)[:, tiles, :],
-                )
+            k_view = k_mix[bi, hi].rearrange("(n p) d -> p n d", p=P)
             q_sb[h] = inputs.tile([P, Q_TILES, HS], BF16, name="q_sb%d" % h)
-            nc.sync.dma_start(out=q_sb[h][:], in_=q[bi, hi].rearrange("(p n) d -> p n d", n=Q_TILES))
+            q_view = q[bi, hi].rearrange("(p n) d -> p n d", n=Q_TILES)
             v_sb[h] = inputs.tile([P, CHUNKS, PACK, HS], BF16, name="v_sb%d" % h)
-            nc.sync.dma_start(
-                out=v_sb[h][:], in_=v_heads[bi, hi].rearrange("(c p j) d -> p c j d", p=P, j=PACK)
-            )
+            v_view = v_heads[bi, hi].rearrange("(c p j) d -> p c j d", p=P, j=PACK)
+            if h == 0:
+                first, second = slice(0, Q_TILES // 2), slice(Q_TILES // 2, Q_TILES)
+                loads = [
+                    (q_sb[h][:, first, :], q_view[:, first, :]),
+                    (k_sb[h][:, first, :], k_view[:, first, :]),
+                    (k_sb[h][:, second, :], k_view[:, second, :]),
+                    (q_sb[h][:, second, :], q_view[:, second, :]),
+                ]
+            else:
+                loads = [(k_sb[h][:], k_view), (q_sb[h][:], q_view)]
+            for tile, view in loads + [(v_sb[h][:], v_view)]:
+                nc.sync.dma_start(out=tile, in_=view)
 
         load_head(0)
 
@@ -143,11 +148,11 @@ def tile_causalselfattention_pb_t_e_kernel(
 
         def mix_chunk(h, c):
             codes, scales = v_mx[h]
-            vm_ps[h] = bank([P, PACK, HS], F32, "vm_ps")
+            vm_ps[h, c] = bank([P, PACK, HS], F32, "vm_ps")
             for t in range(PACK):
                 m_cols = slice(t * P, (t + 1) * P)
                 nc.tensor.matmul_mx(
-                    out=vm_ps[h][:, t, :],
+                    out=vm_ps[h, c][:, t, :],
                     lhsT=w_words[:, c, m_cols].bitcast(FP8X4),
                     lhsT_scale=w_scales[:, c, m_cols],
                     rhs=codes[:, c, :].bitcast(FP8X4),
@@ -157,12 +162,22 @@ def tile_causalselfattention_pb_t_e_kernel(
                 )
 
         def add_bias(h, c):
+            if c == 0:
+                vm_grouped[h] = head.tile(
+                    [P, CHUNKS, HS, PACK], BF16, tag="vm_grouped", name="vm_grouped", align_bytes=64
+                )
             nc.vector.tensor_tensor(
                 out=vm_grouped[h][:, c, :, :],
-                in0=vm_ps[h][:].rearrange("p t d -> p d t"),
+                in0=vm_ps[h, c][:].rearrange("p t d -> p d t"),
                 in1=bias[:, c * PACK : (c + 1) * PACK].unsqueeze(1).to_broadcast([P, HS, PACK]),
                 op=ALU.add,
             )
+
+        def quantise_v(h):
+            v_mx[h] = quantise_values(v_grouped[h], "v")
+
+        def quantise_vm(h):
+            vm_mx[h] = quantise_values(vm_grouped[h], "vm")
 
         def prepare(h, when):
             if when == -8:
@@ -173,20 +188,28 @@ def tile_causalselfattention_pb_t_e_kernel(
                 tokens_ps[h] = transpose_tokens(q_sb[h], ALL_TILES)
             if when == -5:
                 keep_transposed(tokens_ps[h], qT, "qT", h, ALL_TILES, nc.scalar.copy)
-                v_mx[h] = quantise_values(v_grouped[h], "v")
+                quantise_v(h)
             if when == -4:
                 mix_chunk(h, 0)
             if when == -3:
-                vm_grouped[h] = head.tile(
-                    [P, CHUNKS, HS, PACK], BF16, tag="vm_grouped", name="vm_grouped", align_bytes=64
-                )
                 add_bias(h, 0)
             if when == -2:
                 mix_chunk(h, 1)
             if when == -1:
                 add_bias(h, 1)
             if when == 0:
-                vm_mx[h] = quantise_values(vm_grouped[h], "vm")
+                quantise_vm(h)
+
+        def prepare_first(when):
+            if when == 0:
+                quantise_v(0)
+            if when == 1:
+                mix_chunk(0, 0)
+                add_bias(0, 0)
+                mix_chunk(0, 1)
+            if when == 2:
+                add_bias(0, 1)
+                quantise_vm(0)
 
         s_ps, half_max, shift, e_sb, eT_ps, e_grouped, e_mx = {}, {}, {}, {}, {}, {}, {}
 
@@ -289,13 +312,22 @@ def tile_causalselfattention_pb_t_e_kernel(
             h, half = divmod(group, Q_TILES // Y_GROUP)
             first_n = half * Y_GROUP
             bi, hi = divmod(h, NH)
-            y_sb = work.tile([P, Y_GROUP, HS], F32, tag="y_sb")
-            nc.vector.tensor_tensor(
-                out=y_sb[:],
-                in0=y_ps[group][:],
-                in1=inv_sum[group][:].unsqueeze(2).to_broadcast([P, Y_GROUP, HS]),
-                op=ALU.mult,
-            )
+            y_sb = work.tile([P, Y_GROUP, HS], F32, tag="y_sb", name="y_sb")
+            if group % SCALAR_EVERY == SCALAR_EVERY - 2:
+                for j in range(Y_GROUP):
+                    nc.scalar.activation(
+                        out=y_sb[:, j, :],
+                        in_=y_ps[group][:, j, :],
+                        func=ACT.Copy,
+                        scale=inv_sum[group][:, j : j + 1],
+                    )
+            else:
+                nc.vector.tensor_tensor(
+                    out=y_sb[:],
+                    in0=y_ps[group][:],
+                    in1=inv_sum[group][:].unsqueeze(2).to_broadcast([P, Y_GROUP, HS]),
+                    op=ALU.mult,
+                )
             nc.sync.dma_start(
                 out=out[bi].rearrange("(p n) c -> p n c", n=Q_TILES)[
                     :, first_n : first_n + Y_GROUP, hi * HS : (hi + 1) * HS
@@ -305,9 +337,9 @@ def tile_causalselfattention_pb_t_e_kernel(
 
         for piece in range(V_PIECES):
             regroup_v(0, piece)
-        for tiles, copy in ((FIRST_HALF, nc.scalar.copy), (SECOND_HALF, nc.vector.tensor_copy)):
-            keep_transposed(transpose_tokens(k_sb[0], tiles), kT, "kT", 0, tiles, copy)
         keep_transposed(transpose_tokens(q_sb[0], FIRST_HALF), qT, "qT", 0, FIRST_HALF, nc.scalar.copy)
+        for tiles, copy in ((FIRST_HALF, nc.vector.tensor_copy), (SECOND_HALF, nc.scalar.copy)):
+            keep_transposed(transpose_tokens(k_sb[0], tiles), kT, "kT", 0, tiles, copy)
         scores(0)
         row_shift(0)
         keep_transposed(transpose_tokens(q_sb[0], SECOND_HALF), qT, "qT", 0, SECOND_HALF, nc.scalar.copy)
@@ -315,9 +347,6 @@ def tile_causalselfattention_pb_t_e_kernel(
         nc.tensor.transpose(out=b_ps[:, 0:P], in_=b_rows[:], identity=ident_bf[:])
         bias = const.tile([P, CHUNKS * PACK], F32)
         nc.vector.tensor_copy(out=bias[:], in_=b_ps[:, 0 : CHUNKS * PACK])
-        v_mx[0] = quantise_values(v_grouped[0], "v")
-        for when in range(-4, 0):
-            prepare(0, when)
         for piece in range(V_PIECES):
             regroup_v(1, piece)
 
@@ -348,7 +377,9 @@ def tile_causalselfattention_pb_t_e_kernel(
             if ends_group(s - 3):
                 normalise_and_store((s - 3) // Y_GROUP)
             h, j = divmod(s, Q_TILES)
-            if h < HEADS:
+            if h == 0:
+                prepare_first(j)
+            elif h < HEADS:
                 prepare(h, j)
             if h + 1 < HEADS:
                 prepare(h + 1, j - Q_TILES)

@@ -28,7 +28,6 @@ ALL_TILES = range(Q_TILES)
 FIRST_HALF, SECOND_HALF = ALL_TILES[: Q_TILES // 2], ALL_TILES[Q_TILES // 2 :]
 
 V_PIECES = 8
-SCALAR_EVERY = 4
 HEAD_BUFS = 2
 WORK_BUFS = 3
 ROTATING_BANKS = 7
@@ -106,10 +105,10 @@ def tile_causalselfattention_pb_t_e_kernel(
         v_grouped, v_mx, vm_grouped, vm_mx = {}, {}, {}, {}
 
         def transpose_tokens(src, tiles):
-            tokens_ps = bank([P, len(tiles) * P], BF16, "tokens_ps")
-            for i, n in enumerate(tiles):
+            tokens_ps = bank([P, T], BF16, "tokens_ps")
+            for n in tiles:
                 nc.tensor.transpose(
-                    out=tokens_ps[:, i * P : (i + 1) * P], in_=src[:, n, :], identity=ident_bf[:]
+                    out=tokens_ps[:, n * P : (n + 1) * P], in_=src[:, n, :], identity=ident_bf[:]
                 )
             return tokens_ps
 
@@ -117,7 +116,7 @@ def tile_causalselfattention_pb_t_e_kernel(
             if 0 in tiles:
                 dest[h] = head.tile([P, T], BF16, tag=tag, name=tag)
             cols = slice(tiles[0] * P, (tiles[-1] + 1) * P)
-            copy(out=dest[h][:, cols].bitcast(F32), in_=tokens_ps[:].bitcast(F32))
+            copy(out=dest[h][:, cols].bitcast(F32), in_=tokens_ps[:, cols].bitcast(F32))
 
         def regroup_v(h, piece):
             if piece == 0:
@@ -182,12 +181,12 @@ def tile_causalselfattention_pb_t_e_kernel(
         def prepare(h, when):
             if when == -8:
                 tokens_ps[h] = transpose_tokens(k_sb[h], ALL_TILES)
-            if when == -7:
                 keep_transposed(tokens_ps[h], kT, "kT", h, ALL_TILES, nc.scalar.copy)
             if when == -6:
                 tokens_ps[h] = transpose_tokens(q_sb[h], ALL_TILES)
+                keep_transposed(tokens_ps[h], qT, "qT", h, FIRST_HALF, nc.scalar.copy)
             if when == -5:
-                keep_transposed(tokens_ps[h], qT, "qT", h, ALL_TILES, nc.scalar.copy)
+                keep_transposed(tokens_ps[h], qT, "qT", h, SECOND_HALF, nc.vector.tensor_copy)
                 quantise_v(h)
             if when == -4:
                 mix_chunk(h, 0)
@@ -231,7 +230,7 @@ def tile_causalselfattention_pb_t_e_kernel(
 
         def row_shift(u):
             shift[u] = work.tile([P, 1], F32, tag="shift", name="shift")
-            nc.vector.tensor_scalar(
+            nc.gpsimd.tensor_scalar(
                 out=shift[u][:],
                 in0=half_max[u][:, 0:1],
                 scalar1=half_max[u][:, 1:2],
@@ -300,8 +299,11 @@ def tile_causalselfattention_pb_t_e_kernel(
 
         def add_row_sums(group):
             row_sum[group] = work.tile([P, Y_GROUP], F32, tag="row_sum", name="row_sum")
-            nc.vector.tensor_reduce(
-                out=row_sum[group][:], in_=row_sums[group][:], axis=AXIS_X, op=ALU.add
+            nc.gpsimd.tensor_tensor(
+                out=row_sum[group][:],
+                in0=row_sums[group][:, :, 0],
+                in1=row_sums[group][:, :, 1],
+                op=ALU.add,
             )
 
         def invert_row_sums(group):
@@ -313,21 +315,12 @@ def tile_causalselfattention_pb_t_e_kernel(
             first_n = half * Y_GROUP
             bi, hi = divmod(h, NH)
             y_sb = work.tile([P, Y_GROUP, HS], F32, tag="y_sb", name="y_sb")
-            if group % SCALAR_EVERY == SCALAR_EVERY - 2:
-                for j in range(Y_GROUP):
-                    nc.scalar.activation(
-                        out=y_sb[:, j, :],
-                        in_=y_ps[group][:, j, :],
-                        func=ACT.Copy,
-                        scale=inv_sum[group][:, j : j + 1],
-                    )
-            else:
-                nc.vector.tensor_tensor(
-                    out=y_sb[:],
-                    in0=y_ps[group][:],
-                    in1=inv_sum[group][:].unsqueeze(2).to_broadcast([P, Y_GROUP, HS]),
-                    op=ALU.mult,
-                )
+            nc.vector.tensor_tensor(
+                out=y_sb[:],
+                in0=y_ps[group][:],
+                in1=inv_sum[group][:].unsqueeze(2).to_broadcast([P, Y_GROUP, HS]),
+                op=ALU.mult,
+            )
             nc.sync.dma_start(
                 out=out[bi].rearrange("(p n) c -> p n c", n=Q_TILES)[
                     :, first_n : first_n + Y_GROUP, hi * HS : (hi + 1) * HS
@@ -359,6 +352,8 @@ def tile_causalselfattention_pb_t_e_kernel(
         for s in range(UNITS + 3):
             if is_unit(s + 1):
                 scores(s + 1)
+            if ends_group(s - 3):
+                invert_row_sums((s - 3) // Y_GROUP)
             if is_unit(s - 2):
                 quantise_e(s - 2)
             if is_unit(s + 1):
@@ -372,8 +367,6 @@ def tile_causalselfattention_pb_t_e_kernel(
                 weighted_values(s - 3)
             if ends_group(s - 1):
                 add_row_sums((s - 1) // Y_GROUP)
-            if ends_group(s - 2):
-                invert_row_sums((s - 2) // Y_GROUP)
             if ends_group(s - 3):
                 normalise_and_store((s - 3) // Y_GROUP)
             h, j = divmod(s, Q_TILES)

@@ -105,10 +105,10 @@ def tile_causalselfattention_pb_t_e_kernel(
         v_grouped, v_mx, vm_grouped, vm_mx = {}, {}, {}, {}
 
         def transpose_tokens(src, tiles):
-            tokens_ps = bank([P, T], BF16, "tokens_ps")
-            for n in tiles:
+            tokens_ps = bank([P, len(tiles) * P], BF16, "tokens_ps")
+            for i, n in enumerate(tiles):
                 nc.tensor.transpose(
-                    out=tokens_ps[:, n * P : (n + 1) * P], in_=src[:, n, :], identity=ident_bf[:]
+                    out=tokens_ps[:, i * P : (i + 1) * P], in_=src[:, n, :], identity=ident_bf[:]
                 )
             return tokens_ps
 
@@ -116,7 +116,7 @@ def tile_causalselfattention_pb_t_e_kernel(
             if 0 in tiles:
                 dest[h] = head.tile([P, T], BF16, tag=tag, name=tag)
             cols = slice(tiles[0] * P, (tiles[-1] + 1) * P)
-            copy(out=dest[h][:, cols].bitcast(F32), in_=tokens_ps[:, cols].bitcast(F32))
+            copy(out=dest[h][:, cols].bitcast(F32), in_=tokens_ps[:].bitcast(F32))
 
         def regroup_v(h, piece):
             if piece == 0:
@@ -178,15 +178,16 @@ def tile_causalselfattention_pb_t_e_kernel(
         def quantise_vm(h):
             vm_mx[h] = quantise_values(vm_grouped[h], "vm")
 
-        def prepare(h, when):
+        def prepare_scores(h, when):
             if when == -8:
                 tokens_ps[h] = transpose_tokens(k_sb[h], ALL_TILES)
                 keep_transposed(tokens_ps[h], kT, "kT", h, ALL_TILES, nc.scalar.copy)
             if when == -6:
                 tokens_ps[h] = transpose_tokens(q_sb[h], ALL_TILES)
-                keep_transposed(tokens_ps[h], qT, "qT", h, FIRST_HALF, nc.scalar.copy)
+                keep_transposed(tokens_ps[h], qT, "qT", h, ALL_TILES, nc.scalar.copy)
+
+        def prepare_values(h, when):
             if when == -5:
-                keep_transposed(tokens_ps[h], qT, "qT", h, SECOND_HALF, nc.vector.tensor_copy)
                 quantise_v(h)
             if when == -4:
                 mix_chunk(h, 0)
@@ -230,7 +231,7 @@ def tile_causalselfattention_pb_t_e_kernel(
 
         def row_shift(u):
             shift[u] = work.tile([P, 1], F32, tag="shift", name="shift")
-            nc.gpsimd.tensor_scalar(
+            nc.vector.tensor_scalar(
                 out=shift[u][:],
                 in0=half_max[u][:, 0:1],
                 scalar1=half_max[u][:, 1:2],
@@ -340,8 +341,6 @@ def tile_causalselfattention_pb_t_e_kernel(
         nc.tensor.transpose(out=b_ps[:, 0:P], in_=b_rows[:], identity=ident_bf[:])
         bias = const.tile([P, CHUNKS * PACK], F32)
         nc.vector.tensor_copy(out=bias[:], in_=b_ps[:, 0 : CHUNKS * PACK])
-        for piece in range(V_PIECES):
-            regroup_v(1, piece)
 
         def is_unit(u):
             return 0 <= u < UNITS
@@ -363,18 +362,23 @@ def tile_causalselfattention_pb_t_e_kernel(
             if is_unit(s - 1):
                 transpose_e(s - 1)
                 regroup_e(s - 1)
+            h, j = divmod(s, Q_TILES)
+            if h + 1 < HEADS:
+                prepare_scores(h + 1, j - Q_TILES)
             if is_unit(s - 3):
                 weighted_values(s - 3)
             if ends_group(s - 1):
                 add_row_sums((s - 1) // Y_GROUP)
             if ends_group(s - 3):
                 normalise_and_store((s - 3) // Y_GROUP)
-            h, j = divmod(s, Q_TILES)
             if h == 0:
                 prepare_first(j)
             elif h < HEADS:
-                prepare(h, j)
+                prepare_values(h, j)
             if h + 1 < HEADS:
-                prepare(h + 1, j - Q_TILES)
+                prepare_values(h + 1, j - Q_TILES)
+            if s < 3:
+                for piece in range(3 * s, min(3 * s + 3, V_PIECES)):
+                    regroup_v(1, piece)
             if h + 2 < HEADS:
                 regroup_v(h + 2, j)

@@ -28,6 +28,7 @@ ALL_TILES = range(Q_TILES)
 FIRST_HALF, SECOND_HALF = ALL_TILES[: Q_TILES // 2], ALL_TILES[Q_TILES // 2 :]
 
 V_PIECES = 8
+VECTOR_SHIFTS = 2
 HEAD_BUFS = 2
 WORK_BUFS = 3
 ROTATING_BANKS = 7
@@ -105,10 +106,10 @@ def tile_causalselfattention_pb_t_e_kernel(
         v_grouped, v_mx, vm_grouped, vm_mx = {}, {}, {}, {}
 
         def transpose_tokens(src, tiles):
-            tokens_ps = bank([P, len(tiles) * P], BF16, "tokens_ps")
-            for i, n in enumerate(tiles):
+            tokens_ps = bank([P, T], BF16, "tokens_ps")
+            for n in tiles:
                 nc.tensor.transpose(
-                    out=tokens_ps[:, i * P : (i + 1) * P], in_=src[:, n, :], identity=ident_bf[:]
+                    out=tokens_ps[:, n * P : (n + 1) * P], in_=src[:, n, :], identity=ident_bf[:]
                 )
             return tokens_ps
 
@@ -116,7 +117,7 @@ def tile_causalselfattention_pb_t_e_kernel(
             if 0 in tiles:
                 dest[h] = head.tile([P, T], BF16, tag=tag, name=tag)
             cols = slice(tiles[0] * P, (tiles[-1] + 1) * P)
-            copy(out=dest[h][:, cols].bitcast(F32), in_=tokens_ps[:].bitcast(F32))
+            copy(out=dest[h][:, cols].bitcast(F32), in_=tokens_ps[:, cols].bitcast(F32))
 
         def regroup_v(h, piece):
             if piece == 0:
@@ -184,26 +185,34 @@ def tile_causalselfattention_pb_t_e_kernel(
                 keep_transposed(tokens_ps[h], kT, "kT", h, ALL_TILES, nc.scalar.copy)
             if when == -6:
                 tokens_ps[h] = transpose_tokens(q_sb[h], ALL_TILES)
-                keep_transposed(tokens_ps[h], qT, "qT", h, ALL_TILES, nc.scalar.copy)
+                keep_transposed(tokens_ps[h], qT, "qT", h, FIRST_HALF, nc.scalar.copy)
+            if when == -5:
+                keep_transposed(tokens_ps[h], qT, "qT", h, SECOND_HALF, nc.vector.tensor_copy)
 
         def prepare_values(h, when):
-            if when == -5:
+            if when == (-7 if h > 1 else -5):
                 quantise_v(h)
-            if when == -4:
-                mix_chunk(h, 0)
             if when == -3:
+                mix_chunk(h, 0)
                 add_bias(h, 0)
-            if when == -2:
-                mix_chunk(h, 1)
             if when == -1:
+                mix_chunk(h, 1)
                 add_bias(h, 1)
             if when == 0:
                 quantise_vm(h)
+
+        bias = const.tile([P, CHUNKS * PACK], F32)
+
+        def load_bias():
+            b_ps = bank([P, T], BF16, "b_ps")
+            nc.tensor.transpose(out=b_ps[:, 0:P], in_=b_rows[:], identity=ident_bf[:])
+            nc.vector.tensor_copy(out=bias[:], in_=b_ps[:, 0 : CHUNKS * PACK])
 
         def prepare_first(when):
             if when == 0:
                 quantise_v(0)
             if when == 1:
+                load_bias()
                 mix_chunk(0, 0)
                 add_bias(0, 0)
                 mix_chunk(0, 1)
@@ -231,7 +240,8 @@ def tile_causalselfattention_pb_t_e_kernel(
 
         def row_shift(u):
             shift[u] = work.tile([P, 1], F32, tag="shift", name="shift")
-            nc.vector.tensor_scalar(
+            engine = nc.vector if u % Q_TILES < VECTOR_SHIFTS else nc.gpsimd
+            engine.tensor_scalar(
                 out=shift[u][:],
                 in0=half_max[u][:, 0:1],
                 scalar1=half_max[u][:, 1:2],
@@ -337,11 +347,6 @@ def tile_causalselfattention_pb_t_e_kernel(
         scores(0)
         row_shift(0)
         keep_transposed(transpose_tokens(q_sb[0], SECOND_HALF), qT, "qT", 0, SECOND_HALF, nc.scalar.copy)
-        b_ps = bank([P, T], BF16, "b_ps")
-        nc.tensor.transpose(out=b_ps[:, 0:P], in_=b_rows[:], identity=ident_bf[:])
-        bias = const.tile([P, CHUNKS * PACK], F32)
-        nc.vector.tensor_copy(out=bias[:], in_=b_ps[:, 0 : CHUNKS * PACK])
-
         def is_unit(u):
             return 0 <= u < UNITS
 

from contextlib import ExitStack
import math

import concourse.mybir as mybir
from concourse.masks import make_identity

BF16 = mybir.dt.bfloat16
F32 = mybir.dt.float32
I32 = mybir.dt.int32
U32 = mybir.dt.uint32
U8 = mybir.dt.uint8
FP8X4 = mybir.dt.float8_e4m3fn_x4
ALU = mybir.AluOpType
ACT = mybir.ActivationFunctionType
AXIS_X = mybir.AxisListType.X

P = 128
PACK = 4
K_PASS = P * PACK
B, NH, T, HS = 4, 4, 1024, 128
HEADS = B * NH
CHUNKS = T // K_PASS
Q_TILES = T // P
UNITS = HEADS * Q_TILES
Y_GROUP = 4
SCALE = 1.0 / math.sqrt(HS)
ALL_TILES = range(Q_TILES)
FIRST_HALF, SECOND_HALF = ALL_TILES[: Q_TILES // 2], ALL_TILES[Q_TILES // 2 :]

V_PIECES = 8
VECTOR_SHIFTS = 2
HEAD_BUFS = 2
WORK_BUFS = 3
ROTATING_BANKS = 7

FLOPS = 2 * HEADS * (T * K_PASS * HS + 2 * T * T * HS)


def tile_causalselfattention_pb_t_e_kernel(
    tc, q, k_mix, v_heads, pv_W_words, pv_W_scales, pv_b, out
):
    nc = tc.nc
    with ExitStack() as stack:
        const = stack.enter_context(tc.tile_pool(name="const", bufs=1))
        inputs = stack.enter_context(tc.tile_pool(name="inputs", bufs=1))
        head = stack.enter_context(tc.tile_pool(name="head", bufs=HEAD_BUFS))
        work = stack.enter_context(tc.tile_pool(name="work", bufs=WORK_BUFS))
        psum = stack.enter_context(tc.psum_pool(name="psum", bufs=1))
        stack.enter_context(tc.manual_schedule())

        def bank(shape, dtype, name):
            return psum.tile(shape, dtype, tag="bank", bufs=ROTATING_BANKS, name=name)

        k_sb, q_sb, v_sb = {}, {}, {}

        def load_head(h):
            bi, hi = divmod(h, NH)
            k_sb[h] = inputs.tile([P, Q_TILES, HS], BF16, name="k_sb%d" % h)
            k_view = k_mix[bi, hi].rearrange("(n p) d -> p n d", p=P)
            q_sb[h] = inputs.tile([P, Q_TILES, HS], BF16, name="q_sb%d" % h)
            q_view = q[bi, hi].rearrange("(p n) d -> p n d", n=Q_TILES)
            v_sb[h] = inputs.tile([P, CHUNKS, PACK, HS], BF16, name="v_sb%d" % h)
            v_view = v_heads[bi, hi].rearrange("(c p j) d -> p c j d", p=P, j=PACK)
            if h == 0:
                first, second = slice(0, Q_TILES // 2), slice(Q_TILES // 2, Q_TILES)
                loads = [
                    (q_sb[h][:, first, :], q_view[:, first, :]),
                    (k_sb[h][:, first, :], k_view[:, first, :]),
                    (k_sb[h][:, second, :], k_view[:, second, :]),
                    (q_sb[h][:, second, :], q_view[:, second, :]),
                ]
            else:
                loads = [(k_sb[h][:], k_view), (q_sb[h][:], q_view)]
            for tile, view in loads + [(v_sb[h][:], v_view)]:
                nc.sync.dma_start(out=tile, in_=view)

        load_head(0)

        ident_bf = const.tile([P, P], BF16)
        make_identity(nc, ident_bf[:])
        ident_f32 = const.tile([P, P], F32)
        make_identity(nc, ident_f32[:])

        w_words = const.tile([P, CHUNKS, K_PASS], U32, align_bytes=64)
        w_scales = const.tile([P, CHUNKS, K_PASS], U8, align_bytes=64)
        nc.vector.memset(w_scales[:].bitcast(I32), 0)
        b_rows = const.tile([P, P], BF16)
        nc.vector.memset(b_rows[:], 0.0)
        for c in range(CHUNKS):
            nc.sync.dma_start(
                out=w_words[:, c, :].bitcast(I32),
                in_=pv_W_words[c].rearrange("p m t -> p (m t)").bitcast(I32),
            )
            for quad in range(4):
                nc.sync.dma_start(
                    out=w_scales[32 * quad : 32 * quad + 4, c, :].bitcast(I32),
                    in_=pv_W_scales[c, 4 * quad : 4 * quad + 4, :].bitcast(I32),
                )
        nc.sync.dma_start(
            out=b_rows[0 : CHUNKS * PACK, :], in_=pv_b.rearrange("c (t i) -> (c t) i", i=P)
        )
        for h in range(1, HEADS):
            load_head(h)

        tokens_ps, vm_ps, qT, kT = {}, {}, {}, {}
        v_grouped, v_mx, vm_grouped, vm_mx = {}, {}, {}, {}

        def transpose_tokens(src, tiles):
            tokens_ps = bank([P, T], BF16, "tokens_ps")
            for n in tiles:
                nc.tensor.transpose(
                    out=tokens_ps[:, n * P : (n + 1) * P], in_=src[:, n, :], identity=ident_bf[:]
                )
            return tokens_ps

        def keep_transposed(tokens_ps, dest, tag, h, tiles, copy):
            if 0 in tiles:
                dest[h] = head.tile([P, T], BF16, tag=tag, name=tag)
            cols = slice(tiles[0] * P, (tiles[-1] + 1) * P)
            copy(out=dest[h][:, cols].bitcast(F32), in_=tokens_ps[:, cols].bitcast(F32))

        def regroup_v(h, piece):
            if piece == 0:
                v_grouped[h] = head.tile(
                    [P, CHUNKS, HS, PACK], BF16, tag="v_grouped", name="v_grouped", align_bytes=64
                )
            c, part = divmod(piece, V_PIECES // CHUNKS)
            width = HS * CHUNKS // V_PIECES
            channels = slice(part * width, (part + 1) * width)
            nc.gpsimd.tensor_scalar(
                out=v_grouped[h][:, c, channels, :],
                in0=v_sb[h][:, c, :, channels].rearrange("p j d -> p d j"),
                scalar1=1.0,
                scalar2=0.0,
                op0=ALU.mult,
                op1=ALU.add,
            )

        def quantise_values(grouped, tag):
            codes = head.tile([P, CHUNKS, HS], U32, tag=tag + "_codes", name="codes", align_bytes=64)
            scales = head.tile([P, CHUNKS, HS], U8, tag=tag + "_scales", name="scales", align_bytes=64)
            nc.vector.quantize_mx(
                out=codes[:].rearrange("p c d -> p (c d)").bitcast(FP8X4),
                scales=scales[:].rearrange("p c d -> p (c d)"),
                in_=grouped[:].rearrange("p c d j -> p (c d j)"),
            )
            return codes, scales

        def mix_chunk(h, c):
            codes, scales = v_mx[h]
            vm_ps[h, c] = bank([P, PACK, HS], F32, "vm_ps")
            for t in range(PACK):
                m_cols = slice(t * P, (t + 1) * P)
                nc.tensor.matmul_mx(
                    out=vm_ps[h, c][:, t, :],
                    lhsT=w_words[:, c, m_cols].bitcast(FP8X4),
                    lhsT_scale=w_scales[:, c, m_cols],
                    rhs=codes[:, c, :].bitcast(FP8X4),
                    rhs_scale=scales[:, c, :],
                    start=True,
                    stop=True,
                )

        def add_bias(h, c):
            if c == 0:
                vm_grouped[h] = head.tile(
                    [P, CHUNKS, HS, PACK], BF16, tag="vm_grouped", name="vm_grouped", align_bytes=64
                )
            nc.vector.tensor_tensor(
                out=vm_grouped[h][:, c, :, :],
                in0=vm_ps[h, c][:].rearrange("p t d -> p d t"),
                in1=bias[:, c * PACK : (c + 1) * PACK].unsqueeze(1).to_broadcast([P, HS, PACK]),
                op=ALU.add,
            )

        def quantise_v(h):
            v_mx[h] = quantise_values(v_grouped[h], "v")

        def quantise_vm(h):
            vm_mx[h] = quantise_values(vm_grouped[h], "vm")

        def prepare_scores(h, when):
            if when == -8:
                tokens_ps[h] = transpose_tokens(k_sb[h], ALL_TILES)
                keep_transposed(tokens_ps[h], kT, "kT", h, ALL_TILES, nc.scalar.copy)
            if when == -6:
                tokens_ps[h] = transpose_tokens(q_sb[h], ALL_TILES)
                keep_transposed(tokens_ps[h], qT, "qT", h, FIRST_HALF, nc.scalar.copy)
            if when == -5:
                keep_transposed(tokens_ps[h], qT, "qT", h, SECOND_HALF, nc.vector.tensor_copy)

        def prepare_values(h, when):
            if when == (-7 if h > 1 else -5):
                quantise_v(h)
            if when == -3:
                mix_chunk(h, 0)
                add_bias(h, 0)
            if when == -1:
                mix_chunk(h, 1)
                add_bias(h, 1)
            if when == 0:
                quantise_vm(h)

        bias = const.tile([P, CHUNKS * PACK], F32)

        def load_bias():
            b_ps = bank([P, T], BF16, "b_ps")
            nc.tensor.transpose(out=b_ps[:, 0:P], in_=b_rows[:], identity=ident_bf[:])
            nc.vector.tensor_copy(out=bias[:], in_=b_ps[:, 0 : CHUNKS * PACK])

        def prepare_first(when):
            if when == 0:
                quantise_v(0)
            if when == 1:
                load_bias()
                mix_chunk(0, 0)
                add_bias(0, 0)
                mix_chunk(0, 1)
            if when == 2:
                add_bias(0, 1)
                quantise_vm(0)

        s_ps, half_max, shift, e_sb, eT_ps, e_grouped, e_mx = {}, {}, {}, {}, {}, {}, {}

        def scores(u):
            h, n = divmod(u, Q_TILES)
            half_max[u] = work.tile([P, CHUNKS], F32, tag="half_max", name="half_max")
            for g in range(CHUNKS):
                s_ps[u, g] = bank([P, K_PASS], F32, "s_ps")
                nc.tensor.matmul(
                    out=s_ps[u, g][:],
                    lhsT=qT[h][:, n * P : (n + 1) * P],
                    rhs=kT[h][:, g * K_PASS : (g + 1) * K_PASS],
                    start=True,
                    stop=True,
                )
                nc.vector.tensor_reduce(
                    out=half_max[u][:, g : g + 1], in_=s_ps[u, g][:], axis=AXIS_X, op=ALU.max
                )

        def row_shift(u):
            shift[u] = work.tile([P, 1], F32, tag="shift", name="shift")
            engine = nc.vector if u % Q_TILES < VECTOR_SHIFTS else nc.gpsimd
            engine.tensor_scalar(
                out=shift[u][:],
                in0=half_max[u][:, 0:1],
                scalar1=half_max[u][:, 1:2],
                scalar2=-SCALE,
                op0=ALU.max,
                op1=ALU.mult,
            )

        def exponentials(u):
            group, j = divmod(u, Y_GROUP)
            if j == 0:
                row_sums[group] = work.tile([P, Y_GROUP, CHUNKS], F32, tag="row_sums", name="row_sums")
            e_sb[u] = work.tile([P, T], BF16, tag="e_sb", name="e_sb")
            for g in range(CHUNKS):
                nc.scalar.activation(
                    out=e_sb[u][:, g * K_PASS : (g + 1) * K_PASS].rearrange(
                        "q (w p e) -> q w p e", p=P, e=2
                    ),
                    in_=s_ps[u, g][:].rearrange("q (w e p) -> q w p e", p=P, e=2),
                    func=ACT.Exp,
                    bias=shift[u][:, 0:1],
                    scale=SCALE,
                    accum_out=row_sums[group][:, j, g : g + 1],
                )

        def transpose_e(u):
            eT_ps[u] = bank([P, 2 * CHUNKS, P], F32, "eT_ps")
            e_words = e_sb[u][:].bitcast(F32)
            for w in range(2 * CHUNKS):
                nc.tensor.transpose(
                    out=eT_ps[u][:, w, :], in_=e_words[:, w * P : (w + 1) * P], identity=ident_f32[:]
                )

        def regroup_e(u):
            e_grouped[u] = work.tile([P, T], BF16, tag="e_grouped", name="e_grouped", align_bytes=64)
            nc.scalar.copy(
                out=e_grouped[u][:].bitcast(F32).rearrange("p (g q w) -> p g q w", g=CHUNKS, w=2),
                in_=eT_ps[u][:].rearrange("p (g w) q -> p g q w", w=2),
            )

        def quantise_e(u):
            codes = work.tile([P, CHUNKS * P], U32, tag="e_codes", align_bytes=64)
            scales = work.tile([P, CHUNKS * P], U8, tag="e_scales", align_bytes=64)
            nc.vector.quantize_mx(out=codes[:].bitcast(FP8X4), scales=scales[:], in_=e_grouped[u][:])
            e_mx[u] = (codes, scales)

        def weighted_values(u):
            group, j = divmod(u, Y_GROUP)
            if j == 0:
                y_ps[group] = psum.tile([P, Y_GROUP, HS], F32, tag="y", name="y_ps")
            codes, scales = e_mx[u]
            vm_codes, vm_scales = vm_mx[u // Q_TILES]
            for g in range(CHUNKS):
                q_cols = slice(g * P, (g + 1) * P)
                nc.tensor.matmul_mx(
                    out=y_ps[group][:, j, :],
                    lhsT=codes[:, q_cols].bitcast(FP8X4),
                    lhsT_scale=scales[:, q_cols],
                    rhs=vm_codes[:, g, :].bitcast(FP8X4),
                    rhs_scale=vm_scales[:, g, :],
                    start=(g == 0),
                    stop=(g == CHUNKS - 1),
                )

        y_ps, row_sums, row_sum, inv_sum = {}, {}, {}, {}

        def add_row_sums(group):
            row_sum[group] = work.tile([P, Y_GROUP], F32, tag="row_sum", name="row_sum")
            nc.gpsimd.tensor_tensor(
                out=row_sum[group][:],
                in0=row_sums[group][:, :, 0],
                in1=row_sums[group][:, :, 1],
                op=ALU.add,
            )

        def invert_row_sums(group):
            inv_sum[group] = work.tile([P, Y_GROUP], F32, tag="inv_sum", name="inv_sum")
            nc.vector.reciprocal(out=inv_sum[group][:], in_=row_sum[group][:])

        def normalise_and_store(group):
            h, half = divmod(group, Q_TILES // Y_GROUP)
            first_n = half * Y_GROUP
            bi, hi = divmod(h, NH)
            y_sb = work.tile([P, Y_GROUP, HS], F32, tag="y_sb", name="y_sb")
            nc.vector.tensor_tensor(
                out=y_sb[:],
                in0=y_ps[group][:],
                in1=inv_sum[group][:].unsqueeze(2).to_broadcast([P, Y_GROUP, HS]),
                op=ALU.mult,
            )
            nc.sync.dma_start(
                out=out[bi].rearrange("(p n) c -> p n c", n=Q_TILES)[
                    :, first_n : first_n + Y_GROUP, hi * HS : (hi + 1) * HS
                ],
                in_=y_sb[:],
            )

        for piece in range(V_PIECES):
            regroup_v(0, piece)
        keep_transposed(transpose_tokens(q_sb[0], FIRST_HALF), qT, "qT", 0, FIRST_HALF, nc.scalar.copy)
        for tiles, copy in ((FIRST_HALF, nc.vector.tensor_copy), (SECOND_HALF, nc.scalar.copy)):
            keep_transposed(transpose_tokens(k_sb[0], tiles), kT, "kT", 0, tiles, copy)
        scores(0)
        row_shift(0)
        keep_transposed(transpose_tokens(q_sb[0], SECOND_HALF), qT, "qT", 0, SECOND_HALF, nc.scalar.copy)
        def is_unit(u):
            return 0 <= u < UNITS

        def ends_group(u):
            return is_unit(u) and u % Y_GROUP == Y_GROUP - 1

        for s in range(UNITS + 3):
            if is_unit(s + 1):
                scores(s + 1)
            if ends_group(s - 3):
                invert_row_sums((s - 3) // Y_GROUP)
            if is_unit(s - 2):
                quantise_e(s - 2)
            if is_unit(s + 1):
                row_shift(s + 1)
            if is_unit(s):
                exponentials(s)
            if is_unit(s - 1):
                transpose_e(s - 1)
                regroup_e(s - 1)
            h, j = divmod(s, Q_TILES)
            if h + 1 < HEADS:
                prepare_scores(h + 1, j - Q_TILES)
            if is_unit(s - 3):
                weighted_values(s - 3)
            if ends_group(s - 1):
                add_row_sums((s - 1) // Y_GROUP)
            if ends_group(s - 3):
                normalise_and_store((s - 3) // Y_GROUP)
            if h == 0:
                prepare_first(j)
            elif h < HEADS:
                prepare_values(h, j)
            if h + 1 < HEADS:
                prepare_values(h + 1, j - Q_TILES)
            if s < 3:
                for piece in range(3 * s, min(3 * s + 3, V_PIECES)):
                    regroup_v(1, piece)
            if h + 2 < HEADS:
                regroup_v(h + 2, j)
